import numpy as np
import ml_dtypes


def mxq(x, axis, fmt="e4m3"):
    dtype, down = {"e4m3": (ml_dtypes.float8_e4m3fn, 7), "e5m2": (ml_dtypes.float8_e5m2, 14)}[fmt]
    v = np.moveaxis(np.asarray(x, np.float32).astype(ml_dtypes.bfloat16).astype(np.float64), axis, -1)
    blocks = v.reshape(v.shape[:-1] + (-1, 32))
    amax = np.abs(blocks).max(-1, keepdims=True)
    byte = np.maximum(np.where(amax > 0, np.frexp(amax)[1] - 1 + 127, 0) - down, 1)
    scale = np.exp2(byte - 127.0)
    codes = (blocks / scale).astype(np.float32).astype(dtype).astype(np.float64)
    return np.moveaxis((codes * scale).reshape(v.shape), -1, axis)


WIDE = False


def mx_kscale(k):
    if not WIDE:
        return np.ones(k)
    levels = np.array([10, -10, 5, -5, 0])
    a = np.random.permutation(np.resize(levels, k // 512 * 4)).reshape(k // 512, 4)
    idx = np.arange(k)
    return np.exp2(a[idx // 512, idx % 128 // 32])


BF16 = ml_dtypes.bfloat16


def bf(x):
    return np.asarray(x, np.float32).astype(BF16)


def f64(x):
    return np.asarray(x).astype(np.float64)


D, KW, STRIDE, STACK, B, O = 64, 19, 3, 4, 256, 128
W_IN = D * D
POS = (D - KW) // STRIDE + 1
K = STACK * POS * POS


def build_mask():
    base_new = np.tile(np.arange(KW), KW)
    addition_new = np.repeat(np.arange(KW) * D, KW)
    index_1 = addition_new + base_new
    index_width = np.tile(index_1, POS)
    addition_width = np.repeat(STRIDE * np.arange(POS), KW * KW)
    index_row = index_width + addition_width
    index_column = np.tile(index_row, POS)
    addition_height = np.repeat(STRIDE * D * np.arange(POS), KW * KW * POS)
    index_final = index_column + addition_height
    stack = np.repeat(np.arange(POS * POS), KW * KW)
    block = np.zeros((POS * POS, W_IN))
    block[stack, index_final] = 1.0
    return np.vstack([block] * STACK)


def setup_inputs():
    s, t = mx_kscale(W_IN), mx_kscale(K)
    return {"z": bf(np.random.standard_normal((B, W_IN)) * s),
            "T3": bf(np.random.standard_normal((K, W_IN)) * 0.7 / np.sqrt(KW * KW) / s),
            "mask": bf(build_mask()),
            "x1": bf(np.random.standard_normal((B, K)) * 0.7 * t),
            "x2": bf(np.random.standard_normal((B, K)) * 1.4 * t),
            "C_w": bf(np.random.standard_normal((O, K)) / np.sqrt(K) / t),
            "C_b": bf(np.random.standard_normal(O) * 0.5)}


def reference(z, T3, mask, x1, x2, C_w, C_b):
    zq = mxq(f64(z).reshape(-1, D * D), 1, "e4m3")
    p3 = zq @ mxq(f64(mask) * f64(T3), 1, "e4m3").T
    x3 = 2.0 * p3 * f64(x2) - f64(x1)
    return (mxq(x3, 1, "e4m3") @ mxq(f64(C_w), 1, "e4m3").T) + f64(C_b)

@@ -1,0 +1,377 @@
+from contextlib import ExitStack
+
+import concourse.mybir as mybir
+from concourse.masks import make_identity
+
+F32 = mybir.dt.float32
+BF16 = mybir.dt.bfloat16
+U32 = mybir.dt.uint32
+U8 = mybir.dt.uint8
+I32 = mybir.dt.int32
+FP8X4 = mybir.dt.float8_e4m3fn_x4
+ALU = mybir.AluOpType
+
+P = 128
+B, K1, R, O = 256, 4096, 1024, 128
+CHUNK = 512
+ROWK = 64
+TILE_K = 22 * ROWK
+TILE_STEP = 6 * ROWK
+N_TILES = 8
+PAIR_STEP = 32 * K1 + TILE_STEP
+
+FLOPS = 2 * B * K1 * R + 2 * B * R * O
+BYTES = 2 * B * K1 + 2 * 2 * 856064 + 2 * 2 * B * R + 2 * O * R + 2 * O + 4 * B * O
+
+LOADS = [["wp",0],["wp",1],["z",0],["z",1],["wp",2],["z",2],["x2",0],["wp",3],["z",3],["x1",0],["cw",0]]
+
+
+def first_chunk(m):
+    return (TILE_STEP * m) // CHUNK
+
+
+def n_slots(m):
+    return (TILE_STEP * m + TILE_K - 1) // CHUNK - first_chunk(m) + 1
+
+
+def lead_of(m):
+    return TILE_STEP * m - CHUNK * first_chunk(m)
+
+
+def tile_chebyshev_l3_sparsed32_stack_pb_kernel(tc, z, T3, mask, x1, x2, C_w, C_b, out):
+    nc = tc.nc
+    with ExitStack() as ctx:
+        keep = ctx.enter_context(tc.tile_pool(name="keep", bufs=1))
+        acc = ctx.enter_context(tc.psum_pool(name="acc", bufs=1))
+        trp = ctx.enter_context(tc.psum_pool(name="trp", bufs=4))
+        ctx.enter_context(tc.manual_schedule())
+
+        ident_f = keep.tile([P, P], F32, name="ident_f")
+        ident_b = keep.tile([P, P], BF16, name="ident_b")
+        ones = keep.tile([P, P], BF16, name="ones")
+        brow = keep.tile([P, O], BF16, name="brow")
+        bias_sb = keep.tile([P, O], F32, name="bias_sb")
+
+        z_raw = keep.tile([P, 2 * K1], BF16, name="z_raw")
+        zg = keep.tile([P, 8 * 1024], BF16, name="zg", align_bytes=64)
+        zc = keep.tile([P, 8 * 256], U32, name="zc", align_bytes=64)
+        zs = keep.tile([P, 8 * 256], U8, name="zs", align_bytes=64)
+
+        t3 = [keep.tile([P, 2 * TILE_K], BF16, name="t3_%d" % q) for q in range(N_TILES // 2)]
+        mk = [keep.tile([P, 2 * TILE_K], BF16, name="mk_%d" % q) for q in range(N_TILES // 2)]
+        pr = [keep.tile([P, CHUNK * n_slots(m)], BF16, name="pr_%d" % m) for m in range(N_TILES)]
+        wg = [keep.tile([P, CHUNK * n_slots(m)], BF16, name="wg_%d" % m, align_bytes=64) for m in range(N_TILES)]
+        wc = [keep.tile([P, P * n_slots(m)], U32, name="wc_%d" % m, align_bytes=64) for m in range(N_TILES)]
+        ws = [keep.tile([P, P * n_slots(m)], U8, name="ws_%d" % m, align_bytes=64) for m in range(N_TILES)]
+
+        x1s = keep.tile([P, 2 * R], BF16, name="x1s")
+        x2s = keep.tile([P, 2 * R], BF16, name="x2s")
+        tt = keep.tile([P, 2 * R], F32, name="tt")
+        x3 = keep.tile([P, 2 * R], BF16, name="x3")
+        x3g = keep.tile([P, 2 * 1024], BF16, name="x3g", align_bytes=64)
+        x3c = keep.tile([P, 2 * 256], U32, name="x3c", align_bytes=64)
+        x3s = keep.tile([P, 2 * 256], U8, name="x3s", align_bytes=64)
+
+        cw_raw = keep.tile([P, R], BF16, name="cw_raw")
+        cwg = keep.tile([P, 2 * 512], BF16, name="cwg", align_bytes=64)
+        cwc = keep.tile([P, 2 * P], U32, name="cwc", align_bytes=64)
+        cws = keep.tile([P, 2 * P], U8, name="cws", align_bytes=64)
+        osb = [keep.tile([P, O], F32, name="osb_%d" % h) for h in range(2)]
+
+        p3 = [[acc.tile([P, 512], F32, name="p3_%d_%d" % (h, g)) for g in range(2)] for h in range(2)]
+
+        nc.vector.memset(brow[:], 0.0)
+        nc.scalar.dma_start(out=brow[0:1, :], in_=C_b.unsqueeze(0))
+        make_identity(nc, ident_f[:])
+        make_identity(nc, ident_b[:])
+        nc.vector.memset(ones[:], 1.0)
+        for m in range(N_TILES):
+            end = CHUNK * n_slots(m)
+            if lead_of(m) > 0:
+                nc.vector.memset(pr[m][:, 0:lead_of(m)].bitcast(I32), 0)
+            if lead_of(m) + TILE_K < end:
+                nc.vector.memset(pr[m][:, lead_of(m) + TILE_K:end].bitcast(I32), 0)
+
+        zv = z.rearrange("(h p) k -> p h k", h=2)
+        z_dst = z_raw[:].rearrange("p (h k) -> p h k", h=2)
+
+        def load_w(src, dst, m, n, s):
+            start = (256 * s + 32 * m) * K1 + TILE_STEP * m
+            if n == 1:
+                view = src[256 * s + 32 * m:256 * s + 32 * (m + 1), TILE_STEP * m:TILE_STEP * m + TILE_K]
+                nc.sync.dma_start(out=dst[m // 2][s:P:4, TILE_K * (m % 2):TILE_K * (m % 2 + 1)], in_=view)
+            else:
+                flat = src.rearrange("r k -> (r k)")[start:start + 2 * PAIR_STEP]
+                view = flat.rearrange("(t x) -> t x", t=2)[:, 0:32 * K1].rearrange("t (c k) -> c t k", k=K1)[:, :, 0:TILE_K]
+                nc.sync.dma_start(out=dst[m // 2][s:P:4, :].rearrange("c (t k) -> c t k", t=2), in_=view)
+
+        def load(kind, i):
+            if kind == "z":
+                cols = slice(1024 * i, 1024 * (i + 1))
+                nc.sync.dma_start(out=z_dst[:, :, cols], in_=zv[:, :, cols])
+            elif kind == "zc":
+                cols = slice(512 * i, 512 * (i + 1))
+                nc.sync.dma_start(out=z_dst[:, :, cols], in_=zv[:, :, cols])
+            elif kind == "w":
+                for src, dst in ((T3, t3), (mask, mk)):
+                    for s in range(4):
+                        load_w(src, dst, i, 1, s)
+            elif kind == "wp":
+                for src, dst in ((T3, t3), (mask, mk)):
+                    for s in range(4):
+                        if (256 * s + 64 * i) * K1 + TILE_STEP * 2 * i + 2 * PAIR_STEP <= R * K1:
+                            load_w(src, dst, 2 * i, 2, s)
+                        else:
+                            load_w(src, dst, 2 * i, 1, s)
+                            load_w(src, dst, 2 * i + 1, 1, s)
+            elif kind == "x1":
+                nc.sync.dma_start(out=x1s[:].rearrange("p (h r) -> p h r", h=2), in_=x1.rearrange("(h p) r -> p h r", h=2))
+            elif kind == "x2":
+                nc.sync.dma_start(out=x2s[:].rearrange("p (h r) -> p h r", h=2), in_=x2.rearrange("(h p) r -> p h r", h=2))
+            else:
+                nc.sync.dma_start(out=cw_raw[:], in_=C_w)
+
+        for kind, i in LOADS:
+            load(kind, i)
+
+        z_words = z_raw[:].bitcast(F32)
+        zg_words = zg[:].bitcast(F32)
+
+        def z_transpose(c):
+            bank = trp.tile([P, 512], F32, name="ztr", tag="tr")
+            for u in range(2):
+                for h in range(2):
+                    w0 = 2048 * h + 256 * c + 128 * u
+                    nc.tensor.transpose(bank[:, 256 * u + 128 * h:256 * u + 128 * h + 128], z_words[:, w0:w0 + 128], ident_f[:])
+            nc.scalar.copy(
+                out=zg_words[:, 512 * c:512 * (c + 1)].rearrange("p (b u) -> p b u", u=2),
+                in_=bank[:].rearrange("p (u b) -> p b u", u=2),
+            )
+
+        def z_quantise(c, n):
+            nc.vector.quantize_mx(
+                out=zc[:, 256 * c:256 * (c + n)].bitcast(FP8X4),
+                scales=zs[:, 256 * c:256 * (c + n)],
+                in_=zg[:, 1024 * c:1024 * (c + n)],
+            )
+
+        def w_multiply(m, a, b):
+            lo = max(CHUNK * a, lead_of(m))
+            hi = min(CHUNK * b, lead_of(m) + TILE_K)
+            src = slice(TILE_K * (m % 2) + lo - lead_of(m), TILE_K * (m % 2) + hi - lead_of(m))
+            nc.vector.tensor_tensor(out=pr[m][:, lo:hi], in0=t3[m // 2][:, src], in1=mk[m // 2][:, src], op=ALU.mult)
+
+        def w_transpose(m, a, b):
+            words = pr[m][:].bitcast(F32)
+            dst = wg[m][:].bitcast(F32)
+            ns = b - a
+            bank = trp.tile([P, 512], F32, name="wtr", tag="tr")
+            for i in range(2 * ns):
+                nc.tensor.transpose(bank[:, 128 * i:128 * (i + 1)], words[:, 256 * a + 128 * i:256 * a + 128 * (i + 1)], ident_f[:])
+            nc.scalar.copy(
+                out=dst[:, 256 * a:256 * b].rearrange("p (s r u) -> p s r u", s=ns, u=2),
+                in_=bank[:, 0:256 * ns].rearrange("p (s u r) -> p s r u", s=ns, u=2),
+            )
+
+        def w_quantise(m, a, n):
+            nc.vector.quantize_mx(
+                out=wc[m][:, P * a:P * (a + n)].bitcast(FP8X4),
+                scales=ws[m][:, P * a:P * (a + n)],
+                in_=wg[m][:, CHUNK * a:CHUNK * (a + n)],
+            )
+
+        def passes(m, h, a, b):
+            last = n_slots(m) - 1
+            for sl in range(a, b):
+                c = first_chunk(m) + sl
+                zcols = slice(256 * c + 128 * h, 256 * c + 128 * h + 128)
+                nc.tensor.matmul_mx(
+                    out=p3[h][m // 4][:, P * (m % 4):P * (m % 4 + 1)],
+                    lhsT=zc[:, zcols].bitcast(FP8X4),
+                    lhsT_scale=zs[:, zcols],
+                    rhs=wc[m][:, P * sl:P * (sl + 1)].bitcast(FP8X4),
+                    rhs_scale=ws[m][:, P * sl:P * (sl + 1)],
+                    start=(sl == 0),
+                    stop=(sl == last),
+                )
+
+        def by_r(t, h, m0, m1):
+            return t[:, R * h:R * (h + 1)].rearrange("p (s y) -> p y s", s=4)[:, 32 * m0:32 * m1, :]
+
+        def times_x2(m0, m1, h):
+            cols = slice(P * (m0 % 4), P * (m0 % 4) + P * (m1 - m0))
+            nc.vector.scalar_tensor_tensor(
+                out=tt[:, R * h + P * m0:R * h + P * m1].rearrange("p (y s) -> p y s", s=4),
+                in0=p3[h][m0 // 4][:, cols].rearrange("p (y s) -> p y s", s=4),
+                scalar=2.0,
+                in1=by_r(x2s, h, m0, m1),
+                op0=ALU.mult,
+                op1=ALU.mult,
+            )
+
+        def minus_x1(m0, m1, h):
+            nc.vector.tensor_tensor(
+                out=by_r(x3, h, m0, m1),
+                in0=tt[:, R * h + P * m0:R * h + P * m1].rearrange("p (y s) -> p y s", s=4),
+                in1=by_r(x1s, h, m0, m1),
+                op=ALU.subtract,
+            )
+
+        def bias_rows():
+            bank = trp.tile([P, O], F32, name="bps", tag="tr")
+            nc.tensor.matmul(bank[:], lhsT=ones[:], rhs=brow[:], start=True, stop=True)
+            nc.scalar.copy(out=bias_sb[:], in_=bank[:])
+
+        def cw_prepare():
+            bank = trp.tile([P, R], BF16, name="cwtr", tag="tr")
+            for a in range(8):
+                nc.tensor.transpose(bank[:, P * a:P * (a + 1)], cw_raw[:, P * a:P * (a + 1)], ident_b[:])
+            nc.scalar.copy(
+                out=cwg[:].rearrange("p (g o t) -> p g o t", g=2, t=4),
+                in_=bank[:].rearrange("p (g t o) -> p g o t", g=2, t=4),
+            )
+
+        def cw_quantise():
+            nc.vector.quantize_mx(out=cwc[:].bitcast(FP8X4), scales=cws[:], in_=cwg[:])
+
+        s2 = {}
+
+        def x3_transpose(g, h):
+            for big in range(2):
+                if (big, h) not in s2:
+                    if h == 0:
+                        s2[(big, h)] = acc.tile([P, 512], BF16, name="s2_%d_0" % big, tag="p3_%d_0" % big)
+                    else:
+                        s2[(big, h)] = trp.tile([P, 512], BF16, name="s2_%d_1" % big, tag="tr")
+            for s in range(4):
+                a = 2 * s + g
+                nc.tensor.transpose(s2[(a // 4, h)][:, P * (a % 4):P * (a % 4 + 1)], x3[:, R * h + P * a:R * h + P * (a + 1)], ident_b[:])
+
+        def x3_group(big, h, engine_copy):
+            engine_copy(
+                out=x3g[:, 1024 * h + 512 * big:1024 * h + 512 * (big + 1)].rearrange("p (b t) -> p b t", t=4),
+                in_=s2[(big, h)][:].rearrange("p (t b) -> p b t", t=4),
+            )
+
+        def x3_quantise(h):
+            nc.vector.quantize_mx(
+                out=x3c[:, 256 * h:256 * (h + 1)].bitcast(FP8X4),
+                scales=x3s[:, 256 * h:256 * (h + 1)],
+                in_=x3g[:, 1024 * h:1024 * (h + 1)],
+            )
+
+        def head(h):
+            bank = trp.tile([P, O], F32, name="o2", tag="tr")
+            for big in range(2):
+                cols = slice(256 * h + P * big, 256 * h + P * (big + 1))
+                nc.tensor.matmul_mx(
+                    out=bank[:],
+                    lhsT=x3c[:, cols].bitcast(FP8X4),
+                    lhsT_scale=x3s[:, cols],
+                    rhs=cwc[:, P * big:P * (big + 1)].bitcast(FP8X4),
+                    rhs_scale=cws[:, P * big:P * (big + 1)],
+                    start=(big == 0),
+                    stop=(big == 1),
+                )
+            nc.vector.tensor_tensor(out=osb[h][:], in0=bank[:], in1=bias_sb[:], op=ALU.add)
+            nc.sync.dma_start(out=out[P * h:P * (h + 1), :], in_=osb[h][:])
+
+        bias_rows()
+        w_multiply(0, 0, 3)
+        w_multiply(1, 0, 4)
+        w_transpose(0, 0, 2)
+        w_transpose(0, 2, 3)
+        w_transpose(1, 0, 2)
+        w_transpose(1, 2, 4)
+        w_quantise(0, 0, 2)
+        w_quantise(0, 2, 1)
+        w_multiply(2, 0, 4)
+        w_multiply(3, 0, 3)
+        w_transpose(2, 0, 2)
+        z_transpose(0)
+        z_transpose(1)
+        w_quantise(1, 0, 4)
+        w_transpose(2, 2, 4)
+        z_transpose(2)
+        z_transpose(3)
+        z_quantise(0, 2)
+        w_transpose(3, 0, 2)
+        z_quantise(2, 2)
+        w_quantise(2, 0, 4)
+        w_transpose(3, 2, 3)
+        passes(0, 0, 0, 3)
+        w_multiply(4, 0, 3)
+        passes(0, 1, 0, 3)
+        passes(1, 0, 0, 4)
+        passes(1, 1, 0, 4)
+        w_multiply(5, 0, 4)
+        z_transpose(4)
+        z_transpose(5)
+        w_quantise(3, 0, 2)
+        w_transpose(4, 0, 2)
+        w_quantise(3, 2, 1)
+        w_transpose(5, 0, 2)
+        times_x2(0, 2, 0)
+        w_transpose(5, 2, 4)
+        times_x2(0, 2, 1)
+        w_transpose(4, 2, 3)
+        z_quantise(4, 2)
+        w_quantise(4, 0, 2)
+        passes(2, 0, 0, 4)
+        passes(2, 1, 0, 4)
+        passes(3, 0, 0, 3)
+        w_quantise(5, 0, 4)
+        passes(3, 1, 0, 3)
+        w_multiply(6, 0, 4)
+        w_multiply(7, 0, 3)
+        w_transpose(6, 0, 2)
+        z_transpose(6)
+        w_quantise(4, 2, 1)
+        z_transpose(7)
+        times_x2(2, 4, 0)
+        w_transpose(6, 2, 4)
+        times_x2(2, 4, 1)
+        w_transpose(7, 0, 2)
+        minus_x1(0, 2, 0)
+        minus_x1(0, 2, 1)
+        w_transpose(7, 2, 3)
+        passes(4, 0, 0, 3)
+        minus_x1(2, 4, 0)
+        passes(4, 1, 0, 3)
+        z_quantise(6, 2)
+        cw_prepare()
+        w_quantise(6, 0, 4)
+        x3_transpose(0, 0)
+        passes(5, 0, 0, 4)
+        w_quantise(7, 0, 2)
+        passes(5, 1, 0, 4)
+        w_quantise(7, 2, 1)
+        times_x2(4, 6, 0)
+        passes(6, 0, 0, 4)
+        times_x2(4, 6, 1)
+        passes(6, 1, 0, 4)
+        minus_x1(2, 4, 1)
+        passes(7, 0, 0, 3)
+        passes(7, 1, 0, 3)
+        times_x2(6, 7, 0)
+        times_x2(6, 7, 1)
+        x3_transpose(0, 1)
+        times_x2(7, 8, 0)
+        times_x2(7, 8, 1)
+        minus_x1(4, 6, 0)
+        minus_x1(4, 6, 1)
+        minus_x1(6, 7, 0)
+        minus_x1(6, 7, 1)
+        minus_x1(7, 8, 0)
+        minus_x1(7, 8, 1)
+        x3_transpose(1, 0)
+        cw_quantise()
+        x3_transpose(1, 1)
+        x3_group(1, 0, nc.vector.tensor_copy)
+        x3_group(0, 0, nc.scalar.copy)
+        x3_group(0, 1, nc.scalar.copy)
+        x3_group(1, 1, nc.vector.tensor_copy)
+        x3_quantise(0)
+        x3_quantise(1)
+        head(0)
+        head(1)

@@ -23,7 +23,7 @@ PAIR_STEP = 32 * K1 + TILE_STEP
 FLOPS = 2 * B * K1 * R + 2 * B * R * O
 BYTES = 2 * B * K1 + 2 * 2 * 856064 + 2 * 2 * B * R + 2 * O * R + 2 * O + 4 * B * O
 
-LOADS = [["wp",0],["wp",1],["z",0],["z",1],["wp",2],["z",2],["x2",0],["wp",3],["z",3],["x1",0],["cw",0]]
+LOADS = [["wp",0],["z",0],["z",1],["wp",1],["z",2],["wp",2],["wp",3],["z",3],["x2",0],["cw",0],["x1",0]]
 
 
 def first_chunk(m):
@@ -52,7 +52,7 @@ def tile_chebyshev_l3_sparsed32_stack_pb_kernel(tc, z, T3, mask, x1, x2, C_w, C_
         brow = keep.tile([P, O], BF16, name="brow")
         bias_sb = keep.tile([P, O], F32, name="bias_sb")
 
-        z_raw = keep.tile([P, 2 * K1], BF16, name="z_raw")
+        z_raw = [keep.tile([P, 2 * 1024], BF16, name="z_raw_%d" % j) for j in range(4)]
         zg = keep.tile([P, 8 * 1024], BF16, name="zg", align_bytes=64)
         zc = keep.tile([P, 8 * 256], U32, name="zc", align_bytes=64)
         zs = keep.tile([P, 8 * 256], U8, name="zs", align_bytes=64)
@@ -67,7 +67,7 @@ def tile_chebyshev_l3_sparsed32_stack_pb_kernel(tc, z, T3, mask, x1, x2, C_w, C_
         x1s = keep.tile([P, 2 * R], BF16, name="x1s")
         x2s = keep.tile([P, 2 * R], BF16, name="x2s")
         tt = keep.tile([P, 2 * R], F32, name="tt")
-        x3 = keep.tile([P, 2 * R], BF16, name="x3")
+        x3 = [[keep.tile([P, 512], BF16, name="x3_%d_%d" % (h, g)) for g in range(2)] for h in range(2)]
         x3g = keep.tile([P, 2 * 1024], BF16, name="x3g", align_bytes=64)
         x3c = keep.tile([P, 2 * 256], U32, name="x3c", align_bytes=64)
         x3s = keep.tile([P, 2 * 256], U8, name="x3s", align_bytes=64)
@@ -93,7 +93,6 @@ def tile_chebyshev_l3_sparsed32_stack_pb_kernel(tc, z, T3, mask, x1, x2, C_w, C_
                 nc.vector.memset(pr[m][:, lead_of(m) + TILE_K:end].bitcast(I32), 0)
 
         zv = z.rearrange("(h p) k -> p h k", h=2)
-        z_dst = z_raw[:].rearrange("p (h k) -> p h k", h=2)
 
         def load_w(src, dst, m, n, s):
             start = (256 * s + 32 * m) * K1 + TILE_STEP * m
@@ -108,10 +107,7 @@ def tile_chebyshev_l3_sparsed32_stack_pb_kernel(tc, z, T3, mask, x1, x2, C_w, C_
         def load(kind, i):
             if kind == "z":
                 cols = slice(1024 * i, 1024 * (i + 1))
-                nc.sync.dma_start(out=z_dst[:, :, cols], in_=zv[:, :, cols])
-            elif kind == "zc":
-                cols = slice(512 * i, 512 * (i + 1))
-                nc.sync.dma_start(out=z_dst[:, :, cols], in_=zv[:, :, cols])
+                nc.sync.dma_start(out=z_raw[i][:].rearrange("p (h k) -> p h k", h=2), in_=zv[:, :, cols])
             elif kind == "w":
                 for src, dst in ((T3, t3), (mask, mk)):
                     for s in range(4):
@@ -134,15 +130,14 @@ def tile_chebyshev_l3_sparsed32_stack_pb_kernel(tc, z, T3, mask, x1, x2, C_w, C_
         for kind, i in LOADS:
             load(kind, i)
 
-        z_words = z_raw[:].bitcast(F32)
         zg_words = zg[:].bitcast(F32)
 
         def z_transpose(c):
             bank = trp.tile([P, 512], F32, name="ztr", tag="tr")
             for u in range(2):
                 for h in range(2):
-                    w0 = 2048 * h + 256 * c + 128 * u
-                    nc.tensor.transpose(bank[:, 256 * u + 128 * h:256 * u + 128 * h + 128], z_words[:, w0:w0 + 128], ident_f[:])
+                    w0 = 512 * h + 256 * (c % 2) + 128 * u
+                    nc.tensor.transpose(bank[:, 256 * u + 128 * h:256 * u + 128 * h + 128], z_raw[c // 2][:].bitcast(F32)[:, w0:w0 + 128], ident_f[:])
             nc.scalar.copy(
                 out=zg_words[:, 512 * c:512 * (c + 1)].rearrange("p (b u) -> p b u", u=2),
                 in_=bank[:].rearrange("p (u b) -> p b u", u=2),
@@ -211,7 +206,7 @@ def tile_chebyshev_l3_sparsed32_stack_pb_kernel(tc, z, T3, mask, x1, x2, C_w, C_
 
         def minus_x1(m0, m1, h):
             nc.vector.tensor_tensor(
-                out=by_r(x3, h, m0, m1),
+                out=x3[h][m0 // 4][:].rearrange("p (s y) -> p y s", s=4)[:, 32 * (m0 % 4):32 * (m0 % 4) + 32 * (m1 - m0), :],
                 in0=tt[:, R * h + P * m0:R * h + P * m1].rearrange("p (y s) -> p y s", s=4),
                 in1=by_r(x1s, h, m0, m1),
                 op=ALU.subtract,
@@ -245,7 +240,7 @@ def tile_chebyshev_l3_sparsed32_stack_pb_kernel(tc, z, T3, mask, x1, x2, C_w, C_
                         s2[(big, h)] = trp.tile([P, 512], BF16, name="s2_%d_1" % big, tag="tr")
             for s in range(4):
                 a = 2 * s + g
-                nc.tensor.transpose(s2[(a // 4, h)][:, P * (a % 4):P * (a % 4 + 1)], x3[:, R * h + P * a:R * h + P * (a + 1)], ident_b[:])
+                nc.tensor.transpose(s2[(a // 4, h)][:, P * (a % 4):P * (a % 4 + 1)], x3[h][g][:, P * s:P * (s + 1)], ident_b[:])
 
         def x3_group(big, h, engine_copy):
             engine_copy(
@@ -279,25 +274,27 @@ def tile_chebyshev_l3_sparsed32_stack_pb_kernel(tc, z, T3, mask, x1, x2, C_w, C_
         bias_rows()
         w_multiply(0, 0, 3)
         w_multiply(1, 0, 4)
-        w_transpose(0, 0, 2)
-        w_transpose(0, 2, 3)
-        w_transpose(1, 0, 2)
-        w_transpose(1, 2, 4)
-        w_quantise(0, 0, 2)
-        w_quantise(0, 2, 1)
-        w_multiply(2, 0, 4)
-        w_multiply(3, 0, 3)
-        w_transpose(2, 0, 2)
         z_transpose(0)
         z_transpose(1)
-        w_quantise(1, 0, 4)
-        w_transpose(2, 2, 4)
         z_transpose(2)
         z_transpose(3)
+        w_transpose(0, 0, 2)
         z_quantise(0, 2)
-        w_transpose(3, 0, 2)
+        w_transpose(1, 0, 2)
+        w_transpose(1, 2, 4)
         z_quantise(2, 2)
-        w_quantise(2, 0, 4)
+        w_transpose(0, 2, 3)
+        w_multiply(2, 0, 4)
+        w_multiply(3, 0, 3)
+        z_transpose(4)
+        z_transpose(5)
+        w_quantise(0, 0, 2)
+        w_quantise(0, 2, 1)
+        w_quantise(1, 0, 4)
+        w_transpose(2, 0, 2)
+        w_transpose(2, 2, 4)
+        w_transpose(3, 0, 2)
+        z_quantise(4, 2)
         w_transpose(3, 2, 3)
         passes(0, 0, 0, 3)
         w_multiply(4, 0, 3)
@@ -305,57 +302,55 @@ def tile_chebyshev_l3_sparsed32_stack_pb_kernel(tc, z, T3, mask, x1, x2, C_w, C_
         passes(1, 0, 0, 4)
         passes(1, 1, 0, 4)
         w_multiply(5, 0, 4)
-        z_transpose(4)
-        z_transpose(5)
-        w_quantise(3, 0, 2)
         w_transpose(4, 0, 2)
-        w_quantise(3, 2, 1)
-        w_transpose(5, 0, 2)
-        times_x2(0, 2, 0)
-        w_transpose(5, 2, 4)
-        times_x2(0, 2, 1)
+        w_quantise(2, 0, 4)
         w_transpose(4, 2, 3)
-        z_quantise(4, 2)
+        w_transpose(5, 0, 2)
+        w_quantise(3, 0, 2)
+        w_transpose(5, 2, 4)
+        w_quantise(3, 2, 1)
         w_quantise(4, 0, 2)
         passes(2, 0, 0, 4)
+        w_multiply(6, 0, 4)
         passes(2, 1, 0, 4)
         passes(3, 0, 0, 3)
-        w_quantise(5, 0, 4)
         passes(3, 1, 0, 3)
-        w_multiply(6, 0, 4)
         w_multiply(7, 0, 3)
-        w_transpose(6, 0, 2)
         z_transpose(6)
         w_quantise(4, 2, 1)
         z_transpose(7)
-        times_x2(2, 4, 0)
+        w_quantise(5, 0, 4)
+        w_transpose(6, 0, 2)
+        times_x2(0, 2, 0)
         w_transpose(6, 2, 4)
-        times_x2(2, 4, 1)
+        times_x2(0, 2, 1)
+        times_x2(2, 4, 0)
         w_transpose(7, 0, 2)
-        minus_x1(0, 2, 0)
-        minus_x1(0, 2, 1)
-        w_transpose(7, 2, 3)
-        passes(4, 0, 0, 3)
-        minus_x1(2, 4, 0)
-        passes(4, 1, 0, 3)
         z_quantise(6, 2)
-        cw_prepare()
-        w_quantise(6, 0, 4)
-        x3_transpose(0, 0)
+        w_transpose(7, 2, 3)
+        times_x2(2, 4, 1)
+        passes(4, 0, 0, 3)
+        passes(4, 1, 0, 3)
+        minus_x1(0, 2, 0)
         passes(5, 0, 0, 4)
-        w_quantise(7, 0, 2)
+        w_quantise(6, 0, 4)
         passes(5, 1, 0, 4)
+        cw_prepare()
+        w_quantise(7, 0, 2)
         w_quantise(7, 2, 1)
-        times_x2(4, 6, 0)
+        minus_x1(0, 2, 1)
         passes(6, 0, 0, 4)
-        times_x2(4, 6, 1)
+        minus_x1(2, 4, 0)
         passes(6, 1, 0, 4)
         minus_x1(2, 4, 1)
         passes(7, 0, 0, 3)
+        times_x2(4, 6, 0)
         passes(7, 1, 0, 3)
+        times_x2(4, 6, 1)
+        x3_transpose(0, 0)
         times_x2(6, 7, 0)
-        times_x2(6, 7, 1)
         x3_transpose(0, 1)
+        times_x2(6, 7, 1)
         times_x2(7, 8, 0)
         times_x2(7, 8, 1)
         minus_x1(4, 6, 0)
@@ -364,8 +359,8 @@ def tile_chebyshev_l3_sparsed32_stack_pb_kernel(tc, z, T3, mask, x1, x2, C_w, C_
         minus_x1(6, 7, 1)
         minus_x1(7, 8, 0)
         minus_x1(7, 8, 1)
-        x3_transpose(1, 0)
         cw_quantise()
+        x3_transpose(1, 0)
         x3_transpose(1, 1)
         x3_group(1, 0, nc.vector.tensor_copy)
         x3_group(0, 0, nc.scalar.copy)

@@ -66,8 +66,8 @@ def tile_chebyshev_l3_sparsed32_stack_pb_kernel(tc, z, T3, mask, x1, x2, C_w, C_
 
         x1s = keep.tile([P, 2 * R], BF16, name="x1s")
         x2s = keep.tile([P, 2 * R], BF16, name="x2s")
-        tt = keep.tile([P, 2 * R], F32, name="tt")
-        x3 = [[keep.tile([P, 512], BF16, name="x3_%d_%d" % (h, g)) for g in range(2)] for h in range(2)]
+        tt = [[keep.tile([P, 512], F32, name="tt_%d_%d" % (h, g)) for g in range(2)] for h in range(2)]
+        neg_b = keep.tile([P, P], BF16, name="neg_b")
         x3g = keep.tile([P, 2 * 1024], BF16, name="x3g", align_bytes=64)
         x3c = keep.tile([P, 2 * 256], U32, name="x3c", align_bytes=64)
         x3s = keep.tile([P, 2 * 256], U8, name="x3s", align_bytes=64)
@@ -85,6 +85,7 @@ def tile_chebyshev_l3_sparsed32_stack_pb_kernel(tc, z, T3, mask, x1, x2, C_w, C_
         make_identity(nc, ident_f[:])
         make_identity(nc, ident_b[:])
         nc.vector.memset(ones[:], 1.0)
+        nc.vector.tensor_scalar_mul(out=neg_b[:], in0=ident_b[:], scalar1=-1.0)
         for m in range(N_TILES):
             end = CHUNK * n_slots(m)
             if lead_of(m) > 0:
@@ -196,20 +197,12 @@ def tile_chebyshev_l3_sparsed32_stack_pb_kernel(tc, z, T3, mask, x1, x2, C_w, C_
         def times_x2(m0, m1, h):
             cols = slice(P * (m0 % 4), P * (m0 % 4) + P * (m1 - m0))
             nc.vector.scalar_tensor_tensor(
-                out=tt[:, R * h + P * m0:R * h + P * m1].rearrange("p (y s) -> p y s", s=4),
+                out=tt[h][m0 // 4][:].rearrange("p (s y) -> p y s", s=4)[:, 32 * (m0 % 4):32 * (m0 % 4) + 32 * (m1 - m0), :],
                 in0=p3[h][m0 // 4][:, cols].rearrange("p (y s) -> p y s", s=4),
                 scalar=2.0,
                 in1=by_r(x2s, h, m0, m1),
                 op0=ALU.mult,
                 op1=ALU.mult,
-            )
-
-        def minus_x1(m0, m1, h):
-            nc.vector.tensor_tensor(
-                out=x3[h][m0 // 4][:].rearrange("p (s y) -> p y s", s=4)[:, 32 * (m0 % 4):32 * (m0 % 4) + 32 * (m1 - m0), :],
-                in0=tt[:, R * h + P * m0:R * h + P * m1].rearrange("p (y s) -> p y s", s=4),
-                in1=by_r(x1s, h, m0, m1),
-                op=ALU.subtract,
             )
 
         def bias_rows():
@@ -235,12 +228,14 @@ def tile_chebyshev_l3_sparsed32_stack_pb_kernel(tc, z, T3, mask, x1, x2, C_w, C_
             for big in range(2):
                 if (big, h) not in s2:
                     if h == 0:
-                        s2[(big, h)] = acc.tile([P, 512], BF16, name="s2_%d_0" % big, tag="p3_%d_0" % big)
+                        s2[(big, h)] = acc.tile([P, 512], F32, name="s2_%d_0" % big, tag="p3_%d_0" % big)
                     else:
-                        s2[(big, h)] = trp.tile([P, 512], BF16, name="s2_%d_1" % big, tag="tr")
+                        s2[(big, h)] = trp.tile([P, 512], F32, name="s2_%d_1" % big, tag="tr")
             for s in range(4):
                 a = 2 * s + g
-                nc.tensor.transpose(s2[(a // 4, h)][:, P * (a % 4):P * (a % 4 + 1)], x3[h][g][:, P * s:P * (s + 1)], ident_b[:])
+                block = s2[(a // 4, h)][:, P * (a % 4):P * (a % 4 + 1)]
+                nc.tensor.matmul(block, lhsT=x1s[:, R * h + P * a:R * h + P * (a + 1)], rhs=neg_b[:], start=True, stop=False)
+                nc.tensor.matmul(block, lhsT=tt[h][g][:, P * s:P * (s + 1)], rhs=ident_f[:], is_transpose=True, start=False, stop=True)
 
         def x3_group(big, h, engine_copy):
             engine_copy(
@@ -286,15 +281,15 @@ def tile_chebyshev_l3_sparsed32_stack_pb_kernel(tc, z, T3, mask, x1, x2, C_w, C_
         w_transpose(0, 2, 3)
         w_multiply(2, 0, 4)
         w_multiply(3, 0, 3)
-        z_transpose(4)
-        z_transpose(5)
-        w_quantise(0, 0, 2)
-        w_quantise(0, 2, 1)
-        w_quantise(1, 0, 4)
         w_transpose(2, 0, 2)
         w_transpose(2, 2, 4)
+        w_quantise(0, 0, 2)
+        w_quantise(0, 2, 1)
+        z_transpose(4)
+        w_quantise(1, 0, 4)
+        z_transpose(5)
         w_transpose(3, 0, 2)
-        z_quantise(4, 2)
+        w_quantise(2, 0, 4)
         w_transpose(3, 2, 3)
         passes(0, 0, 0, 3)
         w_multiply(4, 0, 3)
@@ -303,7 +298,7 @@ def tile_chebyshev_l3_sparsed32_stack_pb_kernel(tc, z, T3, mask, x1, x2, C_w, C_
         passes(1, 1, 0, 4)
         w_multiply(5, 0, 4)
         w_transpose(4, 0, 2)
-        w_quantise(2, 0, 4)
+        z_quantise(4, 2)
         w_transpose(4, 2, 3)
         w_transpose(5, 0, 2)
         w_quantise(3, 0, 2)
@@ -331,41 +326,31 @@ def tile_chebyshev_l3_sparsed32_stack_pb_kernel(tc, z, T3, mask, x1, x2, C_w, C_
         times_x2(2, 4, 1)
         passes(4, 0, 0, 3)
         passes(4, 1, 0, 3)
-        minus_x1(0, 2, 0)
         passes(5, 0, 0, 4)
         w_quantise(6, 0, 4)
         passes(5, 1, 0, 4)
-        cw_prepare()
+        x3_transpose(0, 0)
         w_quantise(7, 0, 2)
         w_quantise(7, 2, 1)
-        minus_x1(0, 2, 1)
-        passes(6, 0, 0, 4)
-        minus_x1(2, 4, 0)
-        passes(6, 1, 0, 4)
-        minus_x1(2, 4, 1)
-        passes(7, 0, 0, 3)
         times_x2(4, 6, 0)
-        passes(7, 1, 0, 3)
         times_x2(4, 6, 1)
-        x3_transpose(0, 0)
+        passes(6, 0, 0, 4)
+        passes(6, 1, 0, 4)
         times_x2(6, 7, 0)
         x3_transpose(0, 1)
         times_x2(6, 7, 1)
+        passes(7, 0, 0, 3)
+        passes(7, 1, 0, 3)
         times_x2(7, 8, 0)
+        cw_prepare()
         times_x2(7, 8, 1)
-        minus_x1(4, 6, 0)
-        minus_x1(4, 6, 1)
-        minus_x1(6, 7, 0)
-        minus_x1(6, 7, 1)
-        minus_x1(7, 8, 0)
-        minus_x1(7, 8, 1)
-        cw_quantise()
         x3_transpose(1, 0)
         x3_transpose(1, 1)
         x3_group(1, 0, nc.vector.tensor_copy)
         x3_group(0, 0, nc.scalar.copy)
-        x3_group(0, 1, nc.scalar.copy)
         x3_group(1, 1, nc.vector.tensor_copy)
+        x3_group(0, 1, nc.scalar.copy)
+        cw_quantise()
         x3_quantise(0)
         x3_quantise(1)
         head(0)

@@ -44,7 +44,6 @@ def tile_chebyshev_l3_sparsed32_stack_pb_kernel(tc, z, T3, mask, x1, x2, C_w, C_
         keep = ctx.enter_context(tc.tile_pool(name="keep", bufs=1))
         acc = ctx.enter_context(tc.psum_pool(name="acc", bufs=1))
         trp = ctx.enter_context(tc.psum_pool(name="trp", bufs=4))
-        ctx.enter_context(tc.manual_schedule())
 
         ident_f = keep.tile([P, P], F32, name="ident_f")
         ident_b = keep.tile([P, P], BF16, name="ident_b")
@@ -66,8 +65,8 @@ def tile_chebyshev_l3_sparsed32_stack_pb_kernel(tc, z, T3, mask, x1, x2, C_w, C_
 
         x1s = keep.tile([P, 2 * R], BF16, name="x1s")
         x2s = keep.tile([P, 2 * R], BF16, name="x2s")
-        tt = [[keep.tile([P, 512], F32, name="tt_%d_%d" % (h, g)) for g in range(2)] for h in range(2)]
-        neg_b = keep.tile([P, P], BF16, name="neg_b")
+        tt = keep.tile([P, 2 * R], F32, name="tt")
+        x3 = [[keep.tile([P, 512], BF16, name="x3_%d_%d" % (h, g)) for g in range(2)] for h in range(2)]
         x3g = keep.tile([P, 2 * 1024], BF16, name="x3g", align_bytes=64)
         x3c = keep.tile([P, 2 * 256], U32, name="x3c", align_bytes=64)
         x3s = keep.tile([P, 2 * 256], U8, name="x3s", align_bytes=64)
@@ -85,7 +84,6 @@ def tile_chebyshev_l3_sparsed32_stack_pb_kernel(tc, z, T3, mask, x1, x2, C_w, C_
         make_identity(nc, ident_f[:])
         make_identity(nc, ident_b[:])
         nc.vector.memset(ones[:], 1.0)
-        nc.vector.tensor_scalar_mul(out=neg_b[:], in0=ident_b[:], scalar1=-1.0)
         for m in range(N_TILES):
             end = CHUNK * n_slots(m)
             if lead_of(m) > 0:
@@ -197,12 +195,20 @@ def tile_chebyshev_l3_sparsed32_stack_pb_kernel(tc, z, T3, mask, x1, x2, C_w, C_
         def times_x2(m0, m1, h):
             cols = slice(P * (m0 % 4), P * (m0 % 4) + P * (m1 - m0))
             nc.vector.scalar_tensor_tensor(
-                out=tt[h][m0 // 4][:].rearrange("p (s y) -> p y s", s=4)[:, 32 * (m0 % 4):32 * (m0 % 4) + 32 * (m1 - m0), :],
+                out=tt[:, R * h + P * m0:R * h + P * m1].rearrange("p (y s) -> p y s", s=4),
                 in0=p3[h][m0 // 4][:, cols].rearrange("p (y s) -> p y s", s=4),
                 scalar=2.0,
                 in1=by_r(x2s, h, m0, m1),
                 op0=ALU.mult,
                 op1=ALU.mult,
+            )
+
+        def minus_x1(m0, m1, h):
+            nc.vector.tensor_tensor(
+                out=x3[h][m0 // 4][:].rearrange("p (s y) -> p y s", s=4)[:, 32 * (m0 % 4):32 * (m0 % 4) + 32 * (m1 - m0), :],
+                in0=tt[:, R * h + P * m0:R * h + P * m1].rearrange("p (y s) -> p y s", s=4),
+                in1=by_r(x1s, h, m0, m1),
+                op=ALU.subtract,
             )
 
         def bias_rows():
@@ -228,14 +234,12 @@ def tile_chebyshev_l3_sparsed32_stack_pb_kernel(tc, z, T3, mask, x1, x2, C_w, C_
             for big in range(2):
                 if (big, h) not in s2:
                     if h == 0:
-                        s2[(big, h)] = acc.tile([P, 512], F32, name="s2_%d_0" % big, tag="p3_%d_0" % big)
+                        s2[(big, h)] = acc.tile([P, 512], BF16, name="s2_%d_0" % big, tag="p3_%d_0" % big)
                     else:
-                        s2[(big, h)] = trp.tile([P, 512], F32, name="s2_%d_1" % big, tag="tr")
+                        s2[(big, h)] = trp.tile([P, 512], BF16, name="s2_%d_1" % big, tag="tr")
             for s in range(4):
                 a = 2 * s + g
-                block = s2[(a // 4, h)][:, P * (a % 4):P * (a % 4 + 1)]
-                nc.tensor.matmul(block, lhsT=x1s[:, R * h + P * a:R * h + P * (a + 1)], rhs=neg_b[:], start=True, stop=False)
-                nc.tensor.matmul(block, lhsT=tt[h][g][:, P * s:P * (s + 1)], rhs=ident_f[:], is_transpose=True, start=False, stop=True)
+                nc.tensor.transpose(s2[(a // 4, h)][:, P * (a % 4):P * (a % 4 + 1)], x3[h][g][:, P * s:P * (s + 1)], ident_b[:])
 
         def x3_group(big, h, engine_copy):
             engine_copy(
@@ -281,15 +285,15 @@ def tile_chebyshev_l3_sparsed32_stack_pb_kernel(tc, z, T3, mask, x1, x2, C_w, C_
         w_transpose(0, 2, 3)
         w_multiply(2, 0, 4)
         w_multiply(3, 0, 3)
-        w_transpose(2, 0, 2)
-        w_transpose(2, 2, 4)
+        z_transpose(4)
+        z_transpose(5)
         w_quantise(0, 0, 2)
         w_quantise(0, 2, 1)
-        z_transpose(4)
         w_quantise(1, 0, 4)
-        z_transpose(5)
+        w_transpose(2, 0, 2)
+        w_transpose(2, 2, 4)
         w_transpose(3, 0, 2)
-        w_quantise(2, 0, 4)
+        z_quantise(4, 2)
         w_transpose(3, 2, 3)
         passes(0, 0, 0, 3)
         w_multiply(4, 0, 3)
@@ -298,7 +302,7 @@ def tile_chebyshev_l3_sparsed32_stack_pb_kernel(tc, z, T3, mask, x1, x2, C_w, C_
         passes(1, 1, 0, 4)
         w_multiply(5, 0, 4)
         w_transpose(4, 0, 2)
-        z_quantise(4, 2)
+        w_quantise(2, 0, 4)
         w_transpose(4, 2, 3)
         w_transpose(5, 0, 2)
         w_quantise(3, 0, 2)
@@ -326,31 +330,41 @@ def tile_chebyshev_l3_sparsed32_stack_pb_kernel(tc, z, T3, mask, x1, x2, C_w, C_
         times_x2(2, 4, 1)
         passes(4, 0, 0, 3)
         passes(4, 1, 0, 3)
+        minus_x1(0, 2, 0)
         passes(5, 0, 0, 4)
         w_quantise(6, 0, 4)
         passes(5, 1, 0, 4)
-        x3_transpose(0, 0)
+        cw_prepare()
         w_quantise(7, 0, 2)
         w_quantise(7, 2, 1)
-        times_x2(4, 6, 0)
-        times_x2(4, 6, 1)
+        minus_x1(0, 2, 1)
         passes(6, 0, 0, 4)
+        minus_x1(2, 4, 0)
         passes(6, 1, 0, 4)
+        minus_x1(2, 4, 1)
+        passes(7, 0, 0, 3)
+        times_x2(4, 6, 0)
+        passes(7, 1, 0, 3)
+        times_x2(4, 6, 1)
+        x3_transpose(0, 0)
         times_x2(6, 7, 0)
         x3_transpose(0, 1)
         times_x2(6, 7, 1)
-        passes(7, 0, 0, 3)
-        passes(7, 1, 0, 3)
         times_x2(7, 8, 0)
-        cw_prepare()
         times_x2(7, 8, 1)
+        minus_x1(4, 6, 0)
+        minus_x1(4, 6, 1)
+        minus_x1(6, 7, 0)
+        minus_x1(6, 7, 1)
+        minus_x1(7, 8, 0)
+        minus_x1(7, 8, 1)
+        cw_quantise()
         x3_transpose(1, 0)
         x3_transpose(1, 1)
         x3_group(1, 0, nc.vector.tensor_copy)
         x3_group(0, 0, nc.scalar.copy)
-        x3_group(1, 1, nc.vector.tensor_copy)
         x3_group(0, 1, nc.scalar.copy)
-        cw_quantise()
+        x3_group(1, 1, nc.vector.tensor_copy)
         x3_quantise(0)
         x3_quantise(1)
         head(0)

@@ -43,7 +43,9 @@ def tile_chebyshev_l3_sparsed32_stack_pb_kernel(tc, z, T3, mask, x1, x2, C_w, C_
     with ExitStack() as ctx:
         keep = ctx.enter_context(tc.tile_pool(name="keep", bufs=1))
         acc = ctx.enter_context(tc.psum_pool(name="acc", bufs=1))
-        trp = ctx.enter_context(tc.psum_pool(name="trp", bufs=4))
+        trp = ctx.enter_context(tc.psum_pool(name="trp", bufs=3))
+        wrm = ctx.enter_context(tc.psum_pool(name="wrm", bufs=1))
+        ctx.enter_context(tc.manual_schedule())
 
         ident_f = keep.tile([P, P], F32, name="ident_f")
         ident_b = keep.tile([P, P], BF16, name="ident_b")
@@ -211,6 +213,19 @@ def tile_chebyshev_l3_sparsed32_stack_pb_kernel(tc, z, T3, mask, x1, x2, C_w, C_
                 op=ALU.subtract,
             )
 
+        def warm(n):
+            for i in range(n):
+                bank = wrm.tile([P, 512], F32, name="warm")
+                nc.tensor.matmul_mx(
+                    out=bank[:],
+                    lhsT=zc[:, 0:P].bitcast(FP8X4),
+                    lhsT_scale=zs[:, 0:P],
+                    rhs=zc[:, 0:512].bitcast(FP8X4),
+                    rhs_scale=zs[:, 0:512],
+                    start=True,
+                    stop=True,
+                )
+
         def bias_rows():
             bank = trp.tile([P, O], F32, name="bps", tag="tr")
             nc.tensor.matmul(bank[:], lhsT=ones[:], rhs=brow[:], start=True, stop=True)
@@ -301,12 +316,15 @@ def tile_chebyshev_l3_sparsed32_stack_pb_kernel(tc, z, T3, mask, x1, x2, C_w, C_
         passes(1, 0, 0, 4)
         passes(1, 1, 0, 4)
         w_multiply(5, 0, 4)
+        warm(3)
         w_transpose(4, 0, 2)
         w_quantise(2, 0, 4)
         w_transpose(4, 2, 3)
+        warm(1)
         w_transpose(5, 0, 2)
         w_quantise(3, 0, 2)
         w_transpose(5, 2, 4)
+        warm(1)
         w_quantise(3, 2, 1)
         w_quantise(4, 0, 2)
         passes(2, 0, 0, 4)
@@ -318,15 +336,18 @@ def tile_chebyshev_l3_sparsed32_stack_pb_kernel(tc, z, T3, mask, x1, x2, C_w, C_
         z_transpose(6)
         w_quantise(4, 2, 1)
         z_transpose(7)
+        warm(1)
         w_quantise(5, 0, 4)
         w_transpose(6, 0, 2)
         times_x2(0, 2, 0)
         w_transpose(6, 2, 4)
+        warm(1)
         times_x2(0, 2, 1)
         times_x2(2, 4, 0)
         w_transpose(7, 0, 2)
         z_quantise(6, 2)
         w_transpose(7, 2, 3)
+        warm(1)
         times_x2(2, 4, 1)
         passes(4, 0, 0, 3)
         passes(4, 1, 0, 3)
@@ -347,6 +368,7 @@ def tile_chebyshev_l3_sparsed32_stack_pb_kernel(tc, z, T3, mask, x1, x2, C_w, C_
         passes(7, 1, 0, 3)
         times_x2(4, 6, 1)
         x3_transpose(0, 0)
+        warm(1)
         times_x2(6, 7, 0)
         x3_transpose(0, 1)
         times_x2(6, 7, 1)
@@ -360,6 +382,7 @@ def tile_chebyshev_l3_sparsed32_stack_pb_kernel(tc, z, T3, mask, x1, x2, C_w, C_
         minus_x1(7, 8, 1)
         cw_quantise()
         x3_transpose(1, 0)
+        warm(1)
         x3_transpose(1, 1)
         x3_group(1, 0, nc.vector.tensor_copy)
         x3_group(0, 0, nc.scalar.copy)

@@ -43,12 +43,13 @@ def tile_chebyshev_l3_sparsed32_stack_pb_kernel(tc, z, T3, mask, x1, x2, C_w, C_
     with ExitStack() as ctx:
         keep = ctx.enter_context(tc.tile_pool(name="keep", bufs=1))
         acc = ctx.enter_context(tc.psum_pool(name="acc", bufs=1))
-        trp = ctx.enter_context(tc.psum_pool(name="trp", bufs=3))
-        wrm = ctx.enter_context(tc.psum_pool(name="wrm", bufs=1))
+        trp = ctx.enter_context(tc.psum_pool(name="trp", bufs=4))
         ctx.enter_context(tc.manual_schedule())
 
         ident_f = keep.tile([P, P], F32, name="ident_f")
+        perm_f = keep.tile([P, P], F32, name="perm_f")
         ident_b = keep.tile([P, P], BF16, name="ident_b")
+        neg_half = keep.tile([P, P], BF16, name="neg_half")
         ones = keep.tile([P, P], BF16, name="ones")
         brow = keep.tile([P, O], BF16, name="brow")
         bias_sb = keep.tile([P, O], F32, name="bias_sb")
@@ -67,8 +68,7 @@ def tile_chebyshev_l3_sparsed32_stack_pb_kernel(tc, z, T3, mask, x1, x2, C_w, C_
 
         x1s = keep.tile([P, 2 * R], BF16, name="x1s")
         x2s = keep.tile([P, 2 * R], BF16, name="x2s")
-        tt = keep.tile([P, 2 * R], F32, name="tt")
-        x3 = [[keep.tile([P, 512], BF16, name="x3_%d_%d" % (h, g)) for g in range(2)] for h in range(2)]
+        tt = [[keep.tile([P, 512], F32, name="tt_%d_%d" % (h, g)) for g in range(2)] for h in range(2)]
         x3g = keep.tile([P, 2 * 1024], BF16, name="x3g", align_bytes=64)
         x3c = keep.tile([P, 2 * 256], U32, name="x3c", align_bytes=64)
         x3s = keep.tile([P, 2 * 256], U8, name="x3s", align_bytes=64)
@@ -86,6 +86,10 @@ def tile_chebyshev_l3_sparsed32_stack_pb_kernel(tc, z, T3, mask, x1, x2, C_w, C_
         make_identity(nc, ident_f[:])
         make_identity(nc, ident_b[:])
         nc.vector.memset(ones[:], 1.0)
+        nc.vector.tensor_copy(
+            out=perm_f[:].rearrange("p (s c) -> p s c", s=4), in_=ident_f[:].rearrange("p (c s) -> p s c", s=4)
+        )
+        nc.vector.tensor_scalar_mul(out=neg_half[:], in0=ident_b[:], scalar1=-0.5)
         for m in range(N_TILES):
             end = CHUNK * n_slots(m)
             if lead_of(m) > 0:
@@ -163,7 +167,7 @@ def tile_chebyshev_l3_sparsed32_stack_pb_kernel(tc, z, T3, mask, x1, x2, C_w, C_
             ns = b - a
             bank = trp.tile([P, 512], F32, name="wtr", tag="tr")
             for i in range(2 * ns):
-                nc.tensor.transpose(bank[:, 128 * i:128 * (i + 1)], words[:, 256 * a + 128 * i:256 * a + 128 * (i + 1)], ident_f[:])
+                nc.tensor.transpose(bank[:, 128 * i:128 * (i + 1)], words[:, 256 * a + 128 * i:256 * a + 128 * (i + 1)], perm_f[:])
             nc.scalar.copy(
                 out=dst[:, 256 * a:256 * b].rearrange("p (s r u) -> p s r u", s=ns, u=2),
                 in_=bank[:, 0:256 * ns].rearrange("p (s u r) -> p s r u", s=ns, u=2),
@@ -191,40 +195,14 @@ def tile_chebyshev_l3_sparsed32_stack_pb_kernel(tc, z, T3, mask, x1, x2, C_w, C_
                     stop=(sl == last),
                 )
 
-        def by_r(t, h, m0, m1):
-            return t[:, R * h:R * (h + 1)].rearrange("p (s y) -> p y s", s=4)[:, 32 * m0:32 * m1, :]
-
         def times_x2(m0, m1, h):
-            cols = slice(P * (m0 % 4), P * (m0 % 4) + P * (m1 - m0))
-            nc.vector.scalar_tensor_tensor(
-                out=tt[:, R * h + P * m0:R * h + P * m1].rearrange("p (y s) -> p y s", s=4),
-                in0=p3[h][m0 // 4][:, cols].rearrange("p (y s) -> p y s", s=4),
-                scalar=2.0,
-                in1=by_r(x2s, h, m0, m1),
-                op0=ALU.mult,
-                op1=ALU.mult,
-            )
-
-        def minus_x1(m0, m1, h):
+            g = m0 // 4
             nc.vector.tensor_tensor(
-                out=x3[h][m0 // 4][:].rearrange("p (s y) -> p y s", s=4)[:, 32 * (m0 % 4):32 * (m0 % 4) + 32 * (m1 - m0), :],
-                in0=tt[:, R * h + P * m0:R * h + P * m1].rearrange("p (y s) -> p y s", s=4),
-                in1=by_r(x1s, h, m0, m1),
-                op=ALU.subtract,
+                out=tt[h][g][:].rearrange("p (s q c) -> p q s c", s=4, q=4)[:, m0 % 4:m0 % 4 + m1 - m0],
+                in0=p3[h][g][:].rearrange("p (q s c) -> p q s c", s=4, q=4)[:, m0 % 4:m0 % 4 + m1 - m0],
+                in1=x2s[:, R * h:R * (h + 1)].rearrange("p (s q c) -> p q s c", s=4, q=8)[:, m0:m1],
+                op=ALU.mult,
             )
-
-        def warm(n):
-            for i in range(n):
-                bank = wrm.tile([P, 512], F32, name="warm")
-                nc.tensor.matmul_mx(
-                    out=bank[:],
-                    lhsT=zc[:, 0:P].bitcast(FP8X4),
-                    lhsT_scale=zs[:, 0:P],
-                    rhs=zc[:, 0:512].bitcast(FP8X4),
-                    rhs_scale=zs[:, 0:512],
-                    start=True,
-                    stop=True,
-                )
 
         def bias_rows():
             bank = trp.tile([P, O], F32, name="bps", tag="tr")
@@ -249,18 +227,22 @@ def tile_chebyshev_l3_sparsed32_stack_pb_kernel(tc, z, T3, mask, x1, x2, C_w, C_
             for big in range(2):
                 if (big, h) not in s2:
                     if h == 0:
-                        s2[(big, h)] = acc.tile([P, 512], BF16, name="s2_%d_0" % big, tag="p3_%d_0" % big)
+                        s2[(big, h)] = acc.tile([P, 512], F32, name="s2_%d_0" % big, tag="p3_%d_0" % big)
                     else:
-                        s2[(big, h)] = trp.tile([P, 512], BF16, name="s2_%d_1" % big, tag="tr")
+                        s2[(big, h)] = trp.tile([P, 512], F32, name="s2_%d_1" % big, tag="tr")
             for s in range(4):
                 a = 2 * s + g
-                nc.tensor.transpose(s2[(a // 4, h)][:, P * (a % 4):P * (a % 4 + 1)], x3[h][g][:, P * s:P * (s + 1)], ident_b[:])
+                block = s2[(a // 4, h)][:, P * (a % 4):P * (a % 4 + 1)]
+                nc.tensor.matmul(block, lhsT=x1s[:, R * h + P * a:R * h + P * (a + 1)], rhs=neg_half[:], start=True, stop=False)
+                nc.tensor.matmul(block, lhsT=tt[h][g][:, P * s:P * (s + 1)], rhs=ident_f[:], is_transpose=True, start=False, stop=True)
 
-        def x3_group(big, h, engine_copy):
-            engine_copy(
-                out=x3g[:, 1024 * h + 512 * big:1024 * h + 512 * (big + 1)].rearrange("p (b t) -> p b t", t=4),
-                in_=s2[(big, h)][:].rearrange("p (t b) -> p b t", t=4),
-            )
+        def x3_group(big, h, on_vector):
+            dst = x3g[:, 1024 * h + 512 * big:1024 * h + 512 * (big + 1)].rearrange("p (b t) -> p b t", t=4)
+            src = s2[(big, h)][:].rearrange("p (t b) -> p b t", t=4)
+            if on_vector:
+                nc.vector.tensor_scalar_mul(out=dst, in0=src, scalar1=2.0)
+            else:
+                nc.scalar.mul(out=dst, in_=src, mul=2.0)
 
         def x3_quantise(h):
             nc.vector.quantize_mx(
@@ -300,15 +282,15 @@ def tile_chebyshev_l3_sparsed32_stack_pb_kernel(tc, z, T3, mask, x1, x2, C_w, C_
         w_transpose(0, 2, 3)
         w_multiply(2, 0, 4)
         w_multiply(3, 0, 3)
-        z_transpose(4)
-        z_transpose(5)
-        w_quantise(0, 0, 2)
-        w_quantise(0, 2, 1)
-        w_quantise(1, 0, 4)
         w_transpose(2, 0, 2)
         w_transpose(2, 2, 4)
+        w_quantise(0, 0, 2)
+        w_quantise(0, 2, 1)
+        z_transpose(4)
+        w_quantise(1, 0, 4)
+        z_transpose(5)
         w_transpose(3, 0, 2)
-        z_quantise(4, 2)
+        w_quantise(2, 0, 4)
         w_transpose(3, 2, 3)
         passes(0, 0, 0, 3)
         w_multiply(4, 0, 3)
@@ -316,15 +298,12 @@ def tile_chebyshev_l3_sparsed32_stack_pb_kernel(tc, z, T3, mask, x1, x2, C_w, C_
         passes(1, 0, 0, 4)
         passes(1, 1, 0, 4)
         w_multiply(5, 0, 4)
-        warm(3)
         w_transpose(4, 0, 2)
-        w_quantise(2, 0, 4)
+        z_quantise(4, 2)
         w_transpose(4, 2, 3)
-        warm(1)
         w_transpose(5, 0, 2)
         w_quantise(3, 0, 2)
         w_transpose(5, 2, 4)
-        warm(1)
         w_quantise(3, 2, 1)
         w_quantise(4, 0, 2)
         passes(2, 0, 0, 4)
@@ -336,58 +315,41 @@ def tile_chebyshev_l3_sparsed32_stack_pb_kernel(tc, z, T3, mask, x1, x2, C_w, C_
         z_transpose(6)
         w_quantise(4, 2, 1)
         z_transpose(7)
-        warm(1)
         w_quantise(5, 0, 4)
         w_transpose(6, 0, 2)
-        times_x2(0, 2, 0)
+        times_x2(0, 4, 0)
         w_transpose(6, 2, 4)
-        warm(1)
-        times_x2(0, 2, 1)
-        times_x2(2, 4, 0)
+        times_x2(0, 4, 1)
         w_transpose(7, 0, 2)
         z_quantise(6, 2)
         w_transpose(7, 2, 3)
-        warm(1)
-        times_x2(2, 4, 1)
         passes(4, 0, 0, 3)
         passes(4, 1, 0, 3)
-        minus_x1(0, 2, 0)
-        passes(5, 0, 0, 4)
         w_quantise(6, 0, 4)
+        passes(5, 0, 0, 4)
         passes(5, 1, 0, 4)
-        cw_prepare()
         w_quantise(7, 0, 2)
-        w_quantise(7, 2, 1)
-        minus_x1(0, 2, 1)
-        passes(6, 0, 0, 4)
-        minus_x1(2, 4, 0)
-        passes(6, 1, 0, 4)
-        minus_x1(2, 4, 1)
-        passes(7, 0, 0, 3)
-        times_x2(4, 6, 0)
-        passes(7, 1, 0, 3)
-        times_x2(4, 6, 1)
         x3_transpose(0, 0)
-        warm(1)
+        w_quantise(7, 2, 1)
+        times_x2(4, 6, 0)
+        times_x2(4, 6, 1)
+        passes(6, 0, 0, 4)
+        passes(6, 1, 0, 4)
         times_x2(6, 7, 0)
         x3_transpose(0, 1)
         times_x2(6, 7, 1)
+        passes(7, 0, 0, 3)
+        passes(7, 1, 0, 3)
         times_x2(7, 8, 0)
+        cw_prepare()
         times_x2(7, 8, 1)
-        minus_x1(4, 6, 0)
-        minus_x1(4, 6, 1)
-        minus_x1(6, 7, 0)
-        minus_x1(6, 7, 1)
-        minus_x1(7, 8, 0)
-        minus_x1(7, 8, 1)
-        cw_quantise()
         x3_transpose(1, 0)
-        warm(1)
         x3_transpose(1, 1)
-        x3_group(1, 0, nc.vector.tensor_copy)
-        x3_group(0, 0, nc.scalar.copy)
-        x3_group(0, 1, nc.scalar.copy)
-        x3_group(1, 1, nc.vector.tensor_copy)
+        x3_group(1, 0, True)
+        x3_group(0, 0, False)
+        x3_group(1, 1, True)
+        x3_group(0, 1, False)
+        cw_quantise()
         x3_quantise(0)
         x3_quantise(1)
         head(0)

@@ -12,30 +12,34 @@ FP8X4 = mybir.dt.float8_e4m3fn_x4
 ALU = mybir.AluOpType
 
 P = 128
-B, K1, R, O = 256, 4096, 1024, 128
-CHUNK = 512
-ROWK = 64
-TILE_K = 22 * ROWK
-TILE_STEP = 6 * ROWK
-N_TILES = 8
-PAIR_STEP = 32 * K1 + TILE_STEP
+B, K, R, O = 256, 4096, 1024, 128
+HALVES = B // P
+PASS = 512
+STACKS = 4
+TILES = 8
+TILE_K = 22 * 64
+TILE_STEP = 6 * 64
+ROWS = P // STACKS
+PAIR_STEP = ROWS * K + TILE_STEP
 
-FLOPS = 2 * B * K1 * R + 2 * B * R * O
-BYTES = 2 * B * K1 + 2 * 2 * 856064 + 2 * 2 * B * R + 2 * O * R + 2 * O + 4 * B * O
+FLOPS = 2 * B * K * R + 2 * B * R * O
+BYTES = 2 * B * K + 2 * 2 * 856064 + 2 * 2 * B * R + 2 * O * R + 2 * O + 4 * B * O
 
-LOADS = [["wp",0],["z",0],["z",1],["wp",1],["z",2],["wp",2],["wp",3],["z",3],["x2",0],["cw",0],["x1",0]]
-
-
-def first_chunk(m):
-    return (TILE_STEP * m) // CHUNK
-
-
-def n_slots(m):
-    return (TILE_STEP * m + TILE_K - 1) // CHUNK - first_chunk(m) + 1
+Z_PASSES = ((0, 1, 2, 3), (4, 5), (), (6, 7), ())
+EARLY_STEPS = ((0, 2), (2, 4))
+LATE_STEPS = ((4, 6), (6, 7), (7, 8))
 
 
-def lead_of(m):
-    return TILE_STEP * m - CHUNK * first_chunk(m)
+def first_pass(m):
+    return (TILE_STEP * m) // PASS
+
+
+def n_passes(m):
+    return (TILE_STEP * m + TILE_K - 1) // PASS - first_pass(m) + 1
+
+
+def lead(m):
+    return TILE_STEP * m - PASS * first_pass(m)
 
 
 def tile_chebyshev_l3_sparsed32_stack_pb_kernel(tc, z, T3, mask, x1, x2, C_w, C_b, out):
@@ -43,314 +47,282 @@ def tile_chebyshev_l3_sparsed32_stack_pb_kernel(tc, z, T3, mask, x1, x2, C_w, C_
     with ExitStack() as ctx:
         keep = ctx.enter_context(tc.tile_pool(name="keep", bufs=1))
         acc = ctx.enter_context(tc.psum_pool(name="acc", bufs=1))
-        trp = ctx.enter_context(tc.psum_pool(name="trp", bufs=4))
+        turn = ctx.enter_context(tc.psum_pool(name="turn", bufs=4))
         ctx.enter_context(tc.manual_schedule())
 
         ident_f = keep.tile([P, P], F32, name="ident_f")
-        perm_f = keep.tile([P, P], F32, name="perm_f")
         ident_b = keep.tile([P, P], BF16, name="ident_b")
-        neg_half = keep.tile([P, P], BF16, name="neg_half")
         ones = keep.tile([P, P], BF16, name="ones")
-        brow = keep.tile([P, O], BF16, name="brow")
-        bias_sb = keep.tile([P, O], F32, name="bias_sb")
+        bias_row = keep.tile([P, O], BF16, name="bias_row")
+        bias_all = keep.tile([P, O], F32, name="bias_all")
 
-        z_raw = [keep.tile([P, 2 * 1024], BF16, name="z_raw_%d" % j) for j in range(4)]
-        zg = keep.tile([P, 8 * 1024], BF16, name="zg", align_bytes=64)
-        zc = keep.tile([P, 8 * 256], U32, name="zc", align_bytes=64)
-        zs = keep.tile([P, 8 * 256], U8, name="zs", align_bytes=64)
+        z_in = [keep.tile([P, HALVES * 2 * PASS], BF16, name="z_in_%d" % j) for j in range(4)]
+        z_grouped = keep.tile([P, 8 * B * 4], BF16, name="z_grouped", align_bytes=64)
+        z_codes = keep.tile([P, 8 * B], U32, name="z_codes", align_bytes=64)
+        z_scales = keep.tile([P, 8 * B], U8, name="z_scales", align_bytes=64)
 
-        t3 = [keep.tile([P, 2 * TILE_K], BF16, name="t3_%d" % q) for q in range(N_TILES // 2)]
-        mk = [keep.tile([P, 2 * TILE_K], BF16, name="mk_%d" % q) for q in range(N_TILES // 2)]
-        pr = [keep.tile([P, CHUNK * n_slots(m)], BF16, name="pr_%d" % m) for m in range(N_TILES)]
-        wg = [keep.tile([P, CHUNK * n_slots(m)], BF16, name="wg_%d" % m, align_bytes=64) for m in range(N_TILES)]
-        wc = [keep.tile([P, P * n_slots(m)], U32, name="wc_%d" % m, align_bytes=64) for m in range(N_TILES)]
-        ws = [keep.tile([P, P * n_slots(m)], U8, name="ws_%d" % m, align_bytes=64) for m in range(N_TILES)]
+        t3_in = [keep.tile([P, 2 * TILE_K], BF16, name="t3_in_%d" % q) for q in range(TILES // 2)]
+        mask_in = [keep.tile([P, 2 * TILE_K], BF16, name="mask_in_%d" % q) for q in range(TILES // 2)]
+        w_masked = [keep.tile([P, PASS * n_passes(m)], BF16, name="w_masked_%d" % m) for m in range(TILES)]
+        w_grouped = [
+            keep.tile([P, PASS * n_passes(m)], BF16, name="w_grouped_%d" % m, align_bytes=64) for m in range(TILES)
+        ]
+        w_codes = [keep.tile([P, P * n_passes(m)], U32, name="w_codes_%d" % m, align_bytes=64) for m in range(TILES)]
+        w_scales = [keep.tile([P, P * n_passes(m)], U8, name="w_scales_%d" % m, align_bytes=64) for m in range(TILES)]
 
-        x1s = keep.tile([P, 2 * R], BF16, name="x1s")
-        x2s = keep.tile([P, 2 * R], BF16, name="x2s")
-        tt = [[keep.tile([P, 512], F32, name="tt_%d_%d" % (h, g)) for g in range(2)] for h in range(2)]
-        x3g = keep.tile([P, 2 * 1024], BF16, name="x3g", align_bytes=64)
-        x3c = keep.tile([P, 2 * 256], U32, name="x3c", align_bytes=64)
-        x3s = keep.tile([P, 2 * 256], U8, name="x3s", align_bytes=64)
+        x1_in = keep.tile([P, HALVES * R], BF16, name="x1_in")
+        x2_in = keep.tile([P, HALVES * R], BF16, name="x2_in")
+        doubled = keep.tile([P, HALVES * R], F32, name="doubled")
+        x3 = [[keep.tile([P, 512], BF16, name="x3_%d_%d" % (h, g)) for g in range(2)] for h in range(HALVES)]
+        x3_grouped = keep.tile([P, HALVES * 2 * PASS], BF16, name="x3_grouped", align_bytes=64)
+        x3_codes = keep.tile([P, HALVES * 2 * P], U32, name="x3_codes", align_bytes=64)
+        x3_scales = keep.tile([P, HALVES * 2 * P], U8, name="x3_scales", align_bytes=64)
 
-        cw_raw = keep.tile([P, R], BF16, name="cw_raw")
-        cwg = keep.tile([P, 2 * 512], BF16, name="cwg", align_bytes=64)
-        cwc = keep.tile([P, 2 * P], U32, name="cwc", align_bytes=64)
-        cws = keep.tile([P, 2 * P], U8, name="cws", align_bytes=64)
-        osb = [keep.tile([P, O], F32, name="osb_%d" % h) for h in range(2)]
+        cw_in = keep.tile([P, R], BF16, name="cw_in")
+        cw_grouped = keep.tile([P, 2 * PASS], BF16, name="cw_grouped", align_bytes=64)
+        cw_codes = keep.tile([P, 2 * P], U32, name="cw_codes", align_bytes=64)
+        cw_scales = keep.tile([P, 2 * P], U8, name="cw_scales", align_bytes=64)
+        result = [keep.tile([P, O], F32, name="result_%d" % h) for h in range(HALVES)]
 
-        p3 = [[acc.tile([P, 512], F32, name="p3_%d_%d" % (h, g)) for g in range(2)] for h in range(2)]
+        p3 = [[acc.tile([P, 512], F32, name="p3_%d_%d" % (h, g)) for g in range(2)] for h in range(HALVES)]
 
-        nc.vector.memset(brow[:], 0.0)
-        nc.scalar.dma_start(out=brow[0:1, :], in_=C_b.unsqueeze(0))
+        nc.vector.memset(bias_row[:], 0.0)
+        nc.scalar.dma_start(out=bias_row[0:1, :], in_=C_b.unsqueeze(0))
         make_identity(nc, ident_f[:])
         make_identity(nc, ident_b[:])
         nc.vector.memset(ones[:], 1.0)
-        nc.vector.tensor_copy(
-            out=perm_f[:].rearrange("p (s c) -> p s c", s=4), in_=ident_f[:].rearrange("p (c s) -> p s c", s=4)
-        )
-        nc.vector.tensor_scalar_mul(out=neg_half[:], in0=ident_b[:], scalar1=-0.5)
-        for m in range(N_TILES):
-            end = CHUNK * n_slots(m)
-            if lead_of(m) > 0:
-                nc.vector.memset(pr[m][:, 0:lead_of(m)].bitcast(I32), 0)
-            if lead_of(m) + TILE_K < end:
-                nc.vector.memset(pr[m][:, lead_of(m) + TILE_K:end].bitcast(I32), 0)
+        for m in range(TILES):
+            if lead(m) > 0:
+                nc.vector.memset(w_masked[m][:, 0:lead(m)].bitcast(I32), 0)
+            if lead(m) + TILE_K < PASS * n_passes(m):
+                nc.vector.memset(w_masked[m][:, lead(m) + TILE_K:PASS * n_passes(m)].bitcast(I32), 0)
 
-        zv = z.rearrange("(h p) k -> p h k", h=2)
+        def load_z(j):
+            cols = slice(2 * PASS * j, 2 * PASS * (j + 1))
+            nc.sync.dma_start(
+                out=z_in[j][:].rearrange("p (h k) -> p h k", h=HALVES),
+                in_=z.rearrange("(h p) k -> p h k", h=HALVES)[:, :, cols],
+            )
 
-        def load_w(src, dst, m, n, s):
-            start = (256 * s + 32 * m) * K1 + TILE_STEP * m
-            if n == 1:
-                view = src[256 * s + 32 * m:256 * s + 32 * (m + 1), TILE_STEP * m:TILE_STEP * m + TILE_K]
-                nc.sync.dma_start(out=dst[m // 2][s:P:4, TILE_K * (m % 2):TILE_K * (m % 2 + 1)], in_=view)
-            else:
-                flat = src.rearrange("r k -> (r k)")[start:start + 2 * PAIR_STEP]
-                view = flat.rearrange("(t x) -> t x", t=2)[:, 0:32 * K1].rearrange("t (c k) -> c t k", k=K1)[:, :, 0:TILE_K]
-                nc.sync.dma_start(out=dst[m // 2][s:P:4, :].rearrange("c (t k) -> c t k", t=2), in_=view)
+        def load_one_tile(src, dst, m, s):
+            rows = slice(256 * s + ROWS * m, 256 * s + ROWS * (m + 1))
+            nc.sync.dma_start(
+                out=dst[m // 2][s:P:STACKS, TILE_K * (m % 2):TILE_K * (m % 2 + 1)],
+                in_=src[rows, TILE_STEP * m:TILE_STEP * m + TILE_K],
+            )
 
-        def load(kind, i):
-            if kind == "z":
-                cols = slice(1024 * i, 1024 * (i + 1))
-                nc.sync.dma_start(out=z_raw[i][:].rearrange("p (h k) -> p h k", h=2), in_=zv[:, :, cols])
-            elif kind == "w":
-                for src, dst in ((T3, t3), (mask, mk)):
-                    for s in range(4):
-                        load_w(src, dst, i, 1, s)
-            elif kind == "wp":
-                for src, dst in ((T3, t3), (mask, mk)):
-                    for s in range(4):
-                        if (256 * s + 64 * i) * K1 + TILE_STEP * 2 * i + 2 * PAIR_STEP <= R * K1:
-                            load_w(src, dst, 2 * i, 2, s)
-                        else:
-                            load_w(src, dst, 2 * i, 1, s)
-                            load_w(src, dst, 2 * i + 1, 1, s)
-            elif kind == "x1":
-                nc.sync.dma_start(out=x1s[:].rearrange("p (h r) -> p h r", h=2), in_=x1.rearrange("(h p) r -> p h r", h=2))
-            elif kind == "x2":
-                nc.sync.dma_start(out=x2s[:].rearrange("p (h r) -> p h r", h=2), in_=x2.rearrange("(h p) r -> p h r", h=2))
-            else:
-                nc.sync.dma_start(out=cw_raw[:], in_=C_w)
+        def load_two_tiles(q):
+            m = 2 * q
+            for src, dst in ((T3, t3_in), (mask, mask_in)):
+                for s in range(STACKS):
+                    start = (256 * s + ROWS * m) * K + TILE_STEP * m
+                    if start + 2 * PAIR_STEP <= R * K:
+                        both = src.rearrange("r k -> (r k)")[start:start + 2 * PAIR_STEP]
+                        both = both.rearrange("(t x) -> t x", t=2)[:, 0:ROWS * K]
+                        both = both.rearrange("t (c k) -> c t k", k=K)[:, :, 0:TILE_K]
+                        nc.sync.dma_start(out=dst[q][s:P:STACKS, :].rearrange("c (t k) -> c t k", t=2), in_=both)
+                    else:
+                        load_one_tile(src, dst, m, s)
+                        load_one_tile(src, dst, m + 1, s)
 
-        for kind, i in LOADS:
-            load(kind, i)
+        def load_halves(dst, src):
+            nc.sync.dma_start(
+                out=dst[:].rearrange("p (h r) -> p h r", h=HALVES), in_=src.rearrange("(h p) r -> p h r", h=HALVES)
+            )
 
-        zg_words = zg[:].bitcast(F32)
+        load_two_tiles(0)
+        load_z(0)
+        load_z(1)
+        load_two_tiles(1)
+        load_z(2)
+        load_two_tiles(2)
+        load_two_tiles(3)
+        load_z(3)
+        load_halves(x2_in, x2)
+        nc.sync.dma_start(out=cw_in[:], in_=C_w)
+        load_halves(x1_in, x1)
 
         def z_transpose(c):
-            bank = trp.tile([P, 512], F32, name="ztr", tag="tr")
+            words = z_in[c // 2][:].bitcast(F32)
+            bank = turn.tile([P, 512], F32, name="z_t", tag="turn")
             for u in range(2):
-                for h in range(2):
-                    w0 = 512 * h + 256 * (c % 2) + 128 * u
-                    nc.tensor.transpose(bank[:, 256 * u + 128 * h:256 * u + 128 * h + 128], z_raw[c // 2][:].bitcast(F32)[:, w0:w0 + 128], ident_f[:])
+                for h in range(HALVES):
+                    first = PASS * h + 256 * (c % 2) + P * u
+                    nc.tensor.transpose(bank[:, B * u + P * h:B * u + P * (h + 1)], words[:, first:first + P], ident_f[:])
             nc.scalar.copy(
-                out=zg_words[:, 512 * c:512 * (c + 1)].rearrange("p (b u) -> p b u", u=2),
+                out=z_grouped[:].bitcast(F32)[:, 2 * B * c:2 * B * (c + 1)].rearrange("p (b u) -> p b u", u=2),
                 in_=bank[:].rearrange("p (u b) -> p b u", u=2),
             )
 
-        def z_quantise(c, n):
+        def z_quantise(c):
             nc.vector.quantize_mx(
-                out=zc[:, 256 * c:256 * (c + n)].bitcast(FP8X4),
-                scales=zs[:, 256 * c:256 * (c + n)],
-                in_=zg[:, 1024 * c:1024 * (c + n)],
+                out=z_codes[:, B * c:B * (c + 2)].bitcast(FP8X4),
+                scales=z_scales[:, B * c:B * (c + 2)],
+                in_=z_grouped[:, 4 * B * c:4 * B * (c + 2)],
             )
 
-        def w_multiply(m, a, b):
-            lo = max(CHUNK * a, lead_of(m))
-            hi = min(CHUNK * b, lead_of(m) + TILE_K)
-            src = slice(TILE_K * (m % 2) + lo - lead_of(m), TILE_K * (m % 2) + hi - lead_of(m))
-            nc.vector.tensor_tensor(out=pr[m][:, lo:hi], in0=t3[m // 2][:, src], in1=mk[m // 2][:, src], op=ALU.mult)
-
-        def w_transpose(m, a, b):
-            words = pr[m][:].bitcast(F32)
-            dst = wg[m][:].bitcast(F32)
-            ns = b - a
-            bank = trp.tile([P, 512], F32, name="wtr", tag="tr")
-            for i in range(2 * ns):
-                nc.tensor.transpose(bank[:, 128 * i:128 * (i + 1)], words[:, 256 * a + 128 * i:256 * a + 128 * (i + 1)], perm_f[:])
-            nc.scalar.copy(
-                out=dst[:, 256 * a:256 * b].rearrange("p (s r u) -> p s r u", s=ns, u=2),
-                in_=bank[:, 0:256 * ns].rearrange("p (s u r) -> p s r u", s=ns, u=2),
-            )
-
-        def w_quantise(m, a, n):
-            nc.vector.quantize_mx(
-                out=wc[m][:, P * a:P * (a + n)].bitcast(FP8X4),
-                scales=ws[m][:, P * a:P * (a + n)],
-                in_=wg[m][:, CHUNK * a:CHUNK * (a + n)],
-            )
-
-        def passes(m, h, a, b):
-            last = n_slots(m) - 1
-            for sl in range(a, b):
-                c = first_chunk(m) + sl
-                zcols = slice(256 * c + 128 * h, 256 * c + 128 * h + 128)
-                nc.tensor.matmul_mx(
-                    out=p3[h][m // 4][:, P * (m % 4):P * (m % 4 + 1)],
-                    lhsT=zc[:, zcols].bitcast(FP8X4),
-                    lhsT_scale=zs[:, zcols],
-                    rhs=wc[m][:, P * sl:P * (sl + 1)].bitcast(FP8X4),
-                    rhs_scale=ws[m][:, P * sl:P * (sl + 1)],
-                    start=(sl == 0),
-                    stop=(sl == last),
-                )
-
-        def times_x2(m0, m1, h):
-            g = m0 // 4
+        def w_multiply(m):
+            cols = slice(TILE_K * (m % 2), TILE_K * (m % 2 + 1))
             nc.vector.tensor_tensor(
-                out=tt[h][g][:].rearrange("p (s q c) -> p q s c", s=4, q=4)[:, m0 % 4:m0 % 4 + m1 - m0],
-                in0=p3[h][g][:].rearrange("p (q s c) -> p q s c", s=4, q=4)[:, m0 % 4:m0 % 4 + m1 - m0],
-                in1=x2s[:, R * h:R * (h + 1)].rearrange("p (s q c) -> p q s c", s=4, q=8)[:, m0:m1],
+                out=w_masked[m][:, lead(m):lead(m) + TILE_K],
+                in0=t3_in[m // 2][:, cols],
+                in1=mask_in[m // 2][:, cols],
                 op=ALU.mult,
             )
 
-        def bias_rows():
-            bank = trp.tile([P, O], F32, name="bps", tag="tr")
-            nc.tensor.matmul(bank[:], lhsT=ones[:], rhs=brow[:], start=True, stop=True)
-            nc.scalar.copy(out=bias_sb[:], in_=bank[:])
+        def w_transpose(m):
+            words = w_masked[m][:].bitcast(F32)
+            grouped = w_grouped[m][:].bitcast(F32)
+            for a in range(0, n_passes(m), 2):
+                n = min(2, n_passes(m) - a)
+                bank = turn.tile([P, 512], F32, name="w_t", tag="turn")
+                for i in range(2 * n):
+                    nc.tensor.transpose(bank[:, P * i:P * (i + 1)], words[:, 256 * a + P * i:256 * a + P * (i + 1)], ident_f[:])
+                nc.scalar.copy(
+                    out=grouped[:, 256 * a:256 * (a + n)].rearrange("p (a r u) -> p a r u", a=n, u=2),
+                    in_=bank[:, 0:256 * n].rearrange("p (a u r) -> p a r u", a=n, u=2),
+                )
 
-        def cw_prepare():
-            bank = trp.tile([P, R], BF16, name="cwtr", tag="tr")
-            for a in range(8):
-                nc.tensor.transpose(bank[:, P * a:P * (a + 1)], cw_raw[:, P * a:P * (a + 1)], ident_b[:])
+        def w_quantise(m):
+            for a, n in ((0, 4),) if n_passes(m) == 4 else ((0, 2), (2, 1)):
+                nc.vector.quantize_mx(
+                    out=w_codes[m][:, P * a:P * (a + n)].bitcast(FP8X4),
+                    scales=w_scales[m][:, P * a:P * (a + n)],
+                    in_=w_grouped[m][:, PASS * a:PASS * (a + n)],
+                )
+
+        def first_product(m):
+            for h in range(HALVES):
+                for a in range(n_passes(m)):
+                    zcols = slice(B * (first_pass(m) + a) + P * h, B * (first_pass(m) + a) + P * (h + 1))
+                    nc.tensor.matmul_mx(
+                        out=p3[h][m // 4][:, P * (m % 4):P * (m % 4 + 1)],
+                        lhsT=z_codes[:, zcols].bitcast(FP8X4),
+                        lhsT_scale=z_scales[:, zcols],
+                        rhs=w_codes[m][:, P * a:P * (a + 1)].bitcast(FP8X4),
+                        rhs_scale=w_scales[m][:, P * a:P * (a + 1)],
+                        start=(a == 0),
+                        stop=(a == n_passes(m) - 1),
+                    )
+
+        def as_p3(t, h, m0, m1):
+            return t[:, R * h:R * (h + 1)].rearrange("p (s y) -> p y s", s=STACKS)[:, ROWS * m0:ROWS * m1, :]
+
+        def times_x2(m0, m1):
+            for h in range(HALVES):
+                nc.vector.scalar_tensor_tensor(
+                    out=doubled[:, R * h + P * m0:R * h + P * m1].rearrange("p (y s) -> p y s", s=STACKS),
+                    in0=p3[h][m0 // 4][:, P * (m0 % 4):P * (m0 % 4) + P * (m1 - m0)].rearrange("p (y s) -> p y s", s=STACKS),
+                    scalar=2.0,
+                    in1=as_p3(x2_in, h, m0, m1),
+                    op0=ALU.mult,
+                    op1=ALU.mult,
+                )
+
+        def minus_x1(m0, m1):
+            for h in range(HALVES):
+                y = slice(ROWS * (m0 % 4), ROWS * (m0 % 4) + ROWS * (m1 - m0))
+                nc.vector.tensor_tensor(
+                    out=x3[h][m0 // 4][:].rearrange("p (s y) -> p y s", s=STACKS)[:, y, :],
+                    in0=doubled[:, R * h + P * m0:R * h + P * m1].rearrange("p (y s) -> p y s", s=STACKS),
+                    in1=as_p3(x1_in, h, m0, m1),
+                    op=ALU.subtract,
+                )
+
+        def spread_bias():
+            bank = turn.tile([P, O], F32, name="bias_t", tag="turn")
+            nc.tensor.matmul(bank[:], lhsT=ones[:], rhs=bias_row[:], start=True, stop=True)
+            nc.scalar.copy(out=bias_all[:], in_=bank[:])
+
+        def cw_transpose():
+            bank = turn.tile([P, R], BF16, name="cw_t", tag="turn")
+            for a in range(R // P):
+                nc.tensor.transpose(bank[:, P * a:P * (a + 1)], cw_in[:, P * a:P * (a + 1)], ident_b[:])
             nc.scalar.copy(
-                out=cwg[:].rearrange("p (g o t) -> p g o t", g=2, t=4),
+                out=cw_grouped[:].rearrange("p (g o t) -> p g o t", g=2, t=4),
                 in_=bank[:].rearrange("p (g t o) -> p g o t", g=2, t=4),
             )
 
         def cw_quantise():
-            nc.vector.quantize_mx(out=cwc[:].bitcast(FP8X4), scales=cws[:], in_=cwg[:])
+            nc.vector.quantize_mx(out=cw_codes[:].bitcast(FP8X4), scales=cw_scales[:], in_=cw_grouped[:])
 
-        s2 = {}
+        x3_t = {}
 
-        def x3_transpose(g, h):
-            for big in range(2):
-                if (big, h) not in s2:
-                    if h == 0:
-                        s2[(big, h)] = acc.tile([P, 512], F32, name="s2_%d_0" % big, tag="p3_%d_0" % big)
-                    else:
-                        s2[(big, h)] = trp.tile([P, 512], F32, name="s2_%d_1" % big, tag="tr")
-            for s in range(4):
-                a = 2 * s + g
-                block = s2[(a // 4, h)][:, P * (a % 4):P * (a % 4 + 1)]
-                nc.tensor.matmul(block, lhsT=x1s[:, R * h + P * a:R * h + P * (a + 1)], rhs=neg_half[:], start=True, stop=False)
-                nc.tensor.matmul(block, lhsT=tt[h][g][:, P * s:P * (s + 1)], rhs=ident_f[:], is_transpose=True, start=False, stop=True)
+        def x3_transpose(g):
+            for h in range(HALVES):
+                for big in range(2):
+                    if (big, h) not in x3_t:
+                        if h == 0:
+                            x3_t[(big, h)] = acc.tile([P, 512], BF16, name="x3_t_%d_0" % big, tag="p3_%d_0" % big)
+                        else:
+                            x3_t[(big, h)] = turn.tile([P, 512], BF16, name="x3_t_%d_1" % big, tag="turn")
+                for s in range(STACKS):
+                    a = 2 * s + g
+                    nc.tensor.transpose(x3_t[(a // 4, h)][:, P * (a % 4):P * (a % 4 + 1)], x3[h][g][:, P * s:P * (s + 1)], ident_b[:])
 
-        def x3_group(big, h, on_vector):
-            dst = x3g[:, 1024 * h + 512 * big:1024 * h + 512 * (big + 1)].rearrange("p (b t) -> p b t", t=4)
-            src = s2[(big, h)][:].rearrange("p (t b) -> p b t", t=4)
-            if on_vector:
-                nc.vector.tensor_scalar_mul(out=dst, in0=src, scalar1=2.0)
-            else:
-                nc.scalar.mul(out=dst, in_=src, mul=2.0)
+        def x3_group(h):
+            for big, copy in ((0, nc.scalar.copy), (1, nc.vector.tensor_copy)):
+                first = 2 * PASS * h + PASS * big
+                copy(
+                    out=x3_grouped[:, first:first + PASS].rearrange("p (b t) -> p b t", t=4),
+                    in_=x3_t[(big, h)][:].rearrange("p (t b) -> p b t", t=4),
+                )
 
         def x3_quantise(h):
             nc.vector.quantize_mx(
-                out=x3c[:, 256 * h:256 * (h + 1)].bitcast(FP8X4),
-                scales=x3s[:, 256 * h:256 * (h + 1)],
-                in_=x3g[:, 1024 * h:1024 * (h + 1)],
+                out=x3_codes[:, 2 * P * h:2 * P * (h + 1)].bitcast(FP8X4),
+                scales=x3_scales[:, 2 * P * h:2 * P * (h + 1)],
+                in_=x3_grouped[:, 2 * PASS * h:2 * PASS * (h + 1)],
             )
 
         def head(h):
-            bank = trp.tile([P, O], F32, name="o2", tag="tr")
+            bank = turn.tile([P, O], F32, name="out_t", tag="turn")
             for big in range(2):
-                cols = slice(256 * h + P * big, 256 * h + P * (big + 1))
+                cols = slice(2 * P * h + P * big, 2 * P * h + P * (big + 1))
                 nc.tensor.matmul_mx(
                     out=bank[:],
-                    lhsT=x3c[:, cols].bitcast(FP8X4),
-                    lhsT_scale=x3s[:, cols],
-                    rhs=cwc[:, P * big:P * (big + 1)].bitcast(FP8X4),
-                    rhs_scale=cws[:, P * big:P * (big + 1)],
+                    lhsT=x3_codes[:, cols].bitcast(FP8X4),
+                    lhsT_scale=x3_scales[:, cols],
+                    rhs=cw_codes[:, P * big:P * (big + 1)].bitcast(FP8X4),
+                    rhs_scale=cw_scales[:, P * big:P * (big + 1)],
                     start=(big == 0),
                     stop=(big == 1),
                 )
-            nc.vector.tensor_tensor(out=osb[h][:], in0=bank[:], in1=bias_sb[:], op=ALU.add)
-            nc.sync.dma_start(out=out[P * h:P * (h + 1), :], in_=osb[h][:])
+            nc.vector.tensor_tensor(out=result[h][:], in0=bank[:], in1=bias_all[:], op=ALU.add)
+            nc.sync.dma_start(out=out[P * h:P * (h + 1), :], in_=result[h][:])
 
-        bias_rows()
-        w_multiply(0, 0, 3)
-        w_multiply(1, 0, 4)
-        z_transpose(0)
-        z_transpose(1)
-        z_transpose(2)
-        z_transpose(3)
-        w_transpose(0, 0, 2)
-        z_quantise(0, 2)
-        w_transpose(1, 0, 2)
-        w_transpose(1, 2, 4)
-        z_quantise(2, 2)
-        w_transpose(0, 2, 3)
-        w_multiply(2, 0, 4)
-        w_multiply(3, 0, 3)
-        w_transpose(2, 0, 2)
-        w_transpose(2, 2, 4)
-        w_quantise(0, 0, 2)
-        w_quantise(0, 2, 1)
-        z_transpose(4)
-        w_quantise(1, 0, 4)
-        z_transpose(5)
-        w_transpose(3, 0, 2)
-        w_quantise(2, 0, 4)
-        w_transpose(3, 2, 3)
-        passes(0, 0, 0, 3)
-        w_multiply(4, 0, 3)
-        passes(0, 1, 0, 3)
-        passes(1, 0, 0, 4)
-        passes(1, 1, 0, 4)
-        w_multiply(5, 0, 4)
-        w_transpose(4, 0, 2)
-        z_quantise(4, 2)
-        w_transpose(4, 2, 3)
-        w_transpose(5, 0, 2)
-        w_quantise(3, 0, 2)
-        w_transpose(5, 2, 4)
-        w_quantise(3, 2, 1)
-        w_quantise(4, 0, 2)
-        passes(2, 0, 0, 4)
-        w_multiply(6, 0, 4)
-        passes(2, 1, 0, 4)
-        passes(3, 0, 0, 3)
-        passes(3, 1, 0, 3)
-        w_multiply(7, 0, 3)
-        z_transpose(6)
-        w_quantise(4, 2, 1)
-        z_transpose(7)
-        w_quantise(5, 0, 4)
-        w_transpose(6, 0, 2)
-        times_x2(0, 4, 0)
-        w_transpose(6, 2, 4)
-        times_x2(0, 4, 1)
-        w_transpose(7, 0, 2)
-        z_quantise(6, 2)
-        w_transpose(7, 2, 3)
-        passes(4, 0, 0, 3)
-        passes(4, 1, 0, 3)
-        w_quantise(6, 0, 4)
-        passes(5, 0, 0, 4)
-        passes(5, 1, 0, 4)
-        w_quantise(7, 0, 2)
-        x3_transpose(0, 0)
-        w_quantise(7, 2, 1)
-        times_x2(4, 6, 0)
-        times_x2(4, 6, 1)
-        passes(6, 0, 0, 4)
-        passes(6, 1, 0, 4)
-        times_x2(6, 7, 0)
-        x3_transpose(0, 1)
-        times_x2(6, 7, 1)
-        passes(7, 0, 0, 3)
-        passes(7, 1, 0, 3)
-        times_x2(7, 8, 0)
-        cw_prepare()
-        times_x2(7, 8, 1)
-        x3_transpose(1, 0)
-        x3_transpose(1, 1)
-        x3_group(1, 0, True)
-        x3_group(0, 0, False)
-        x3_group(1, 1, True)
-        x3_group(0, 1, False)
+        spread_bias()
+        for q in range(TILES // 2 + 1):
+            new = (2 * q, 2 * q + 1) if q < TILES // 2 else ()
+            old = (2 * q - 2, 2 * q - 1) if q > 0 else ()
+            for m in new:
+                w_multiply(m)
+            for c in Z_PASSES[q]:
+                z_transpose(c)
+            for m in new:
+                w_transpose(m)
+            for m in old:
+                w_quantise(m)
+            if q == 3:
+                for m0, m1 in EARLY_STEPS:
+                    times_x2(m0, m1)
+            for c in Z_PASSES[q][::2]:
+                z_quantise(c)
+            for m in old:
+                first_product(m)
+        cw_transpose()
+        for m0, m1 in EARLY_STEPS:
+            minus_x1(m0, m1)
+        x3_transpose(0)
+        for m0, m1 in LATE_STEPS:
+            times_x2(m0, m1)
+        for m0, m1 in LATE_STEPS:
+            minus_x1(m0, m1)
         cw_quantise()
-        x3_quantise(0)
-        x3_quantise(1)
-        head(0)
-        head(1)
+        x3_transpose(1)
+        for h in range(HALVES):
+            x3_group(h)
+        for h in range(HALVES):
+            x3_quantise(h)
+        for h in range(HALVES):
+            head(h)

@@ -26,8 +26,6 @@ FLOPS = 2 * B * K * R + 2 * B * R * O
 BYTES = 2 * B * K + 2 * 2 * 856064 + 2 * 2 * B * R + 2 * O * R + 2 * O + 4 * B * O
 
 Z_PASSES = ((0, 1, 2, 3), (4, 5), (), (6, 7), ())
-EARLY_STEPS = ((0, 2), (2, 4))
-LATE_STEPS = ((4, 6), (6, 7), (7, 8))
 
 
 def first_pass(m):
@@ -72,7 +70,7 @@ def tile_chebyshev_l3_sparsed32_stack_pb_kernel(tc, z, T3, mask, x1, x2, C_w, C_
 
         x1_in = keep.tile([P, HALVES * R], BF16, name="x1_in")
         x2_in = keep.tile([P, HALVES * R], BF16, name="x2_in")
-        doubled = keep.tile([P, HALVES * R], F32, name="doubled")
+        doubled = [[keep.tile([P, 512], F32, name="doubled_%d_%d" % (h, g)) for g in range(2)] for h in range(HALVES)]
         x3 = [[keep.tile([P, 512], BF16, name="x3_%d_%d" % (h, g)) for g in range(2)] for h in range(HALVES)]
         x3_grouped = keep.tile([P, HALVES * 2 * PASS], BF16, name="x3_grouped", align_bytes=64)
         x3_codes = keep.tile([P, HALVES * 2 * P], U32, name="x3_codes", align_bytes=64)
@@ -205,27 +203,26 @@ def tile_chebyshev_l3_sparsed32_stack_pb_kernel(tc, z, T3, mask, x1, x2, C_w, C_
                         stop=(a == n_passes(m) - 1),
                     )
 
-        def as_p3(t, h, m0, m1):
-            return t[:, R * h:R * (h + 1)].rearrange("p (s y) -> p y s", s=STACKS)[:, ROWS * m0:ROWS * m1, :]
+        def as_p3(t, h, g):
+            return t[:, R * h:R * (h + 1)].rearrange("p (s g y) -> p g y s", s=STACKS, g=2)[:, g]
 
-        def times_x2(m0, m1):
+        def times_x2(g):
             for h in range(HALVES):
                 nc.vector.scalar_tensor_tensor(
-                    out=doubled[:, R * h + P * m0:R * h + P * m1].rearrange("p (y s) -> p y s", s=STACKS),
-                    in0=p3[h][m0 // 4][:, P * (m0 % 4):P * (m0 % 4) + P * (m1 - m0)].rearrange("p (y s) -> p y s", s=STACKS),
+                    out=doubled[h][g][:].rearrange("p (y s) -> p y s", s=STACKS),
+                    in0=p3[h][g][:].rearrange("p (y s) -> p y s", s=STACKS),
                     scalar=2.0,
-                    in1=as_p3(x2_in, h, m0, m1),
+                    in1=as_p3(x2_in, h, g),
                     op0=ALU.mult,
                     op1=ALU.mult,
                 )
 
-        def minus_x1(m0, m1):
+        def minus_x1(g):
             for h in range(HALVES):
-                y = slice(ROWS * (m0 % 4), ROWS * (m0 % 4) + ROWS * (m1 - m0))
                 nc.vector.tensor_tensor(
-                    out=x3[h][m0 // 4][:].rearrange("p (s y) -> p y s", s=STACKS)[:, y, :],
-                    in0=doubled[:, R * h + P * m0:R * h + P * m1].rearrange("p (y s) -> p y s", s=STACKS),
-                    in1=as_p3(x1_in, h, m0, m1),
+                    out=x3[h][g][:].rearrange("p (s y) -> p y s", s=STACKS),
+                    in0=doubled[h][g][:].rearrange("p (y s) -> p y s", s=STACKS),
+                    in1=as_p3(x1_in, h, g),
                     op=ALU.subtract,
                 )
 
@@ -304,20 +301,16 @@ def tile_chebyshev_l3_sparsed32_stack_pb_kernel(tc, z, T3, mask, x1, x2, C_w, C_
             for m in old:
                 w_quantise(m)
             if q == 3:
-                for m0, m1 in EARLY_STEPS:
-                    times_x2(m0, m1)
+                times_x2(0)
             for c in Z_PASSES[q][::2]:
                 z_quantise(c)
             for m in old:
                 first_product(m)
         cw_transpose()
-        for m0, m1 in EARLY_STEPS:
-            minus_x1(m0, m1)
+        minus_x1(0)
         x3_transpose(0)
-        for m0, m1 in LATE_STEPS:
-            times_x2(m0, m1)
-        for m0, m1 in LATE_STEPS:
-            minus_x1(m0, m1)
+        times_x2(1)
+        minus_x1(1)
         cw_quantise()
         x3_transpose(1)
         for h in range(HALVES):

@@ -134,7 +134,10 @@ def tile_chebyshev_l3_sparsed32_stack_pb_kernel(tc, z, T3, mask, x1, x2, C_w, C_
         load_two_tiles(1)
         load_z(2)
         load_two_tiles(2)
-        load_two_tiles(3)
+        for m in (6, 7):
+            for src, dst in ((T3, t3_in), (mask, mask_in)):
+                for s in range(STACKS):
+                    load_one_tile(src, dst, m, s)
         load_z(3)
         load_halves(x2_in, x2)
         nc.sync.dma_start(out=cw_in[:], in_=C_w)
@@ -292,14 +295,24 @@ def tile_chebyshev_l3_sparsed32_stack_pb_kernel(tc, z, T3, mask, x1, x2, C_w, C_
         for q in range(TILES // 2 + 1):
             new = (2 * q, 2 * q + 1) if q < TILES // 2 else ()
             old = (2 * q - 2, 2 * q - 1) if q > 0 else ()
-            for m in new:
-                w_multiply(m)
-            for c in Z_PASSES[q]:
-                z_transpose(c)
-            for m in new:
-                w_transpose(m)
-            for m in old:
-                w_quantise(m)
+            if q == 3:
+                w_multiply(6)
+                w_transpose(6)
+                for m in old:
+                    w_quantise(m)
+                w_multiply(7)
+                for c in Z_PASSES[q]:
+                    z_transpose(c)
+                w_transpose(7)
+            else:
+                for m in new:
+                    w_multiply(m)
+                for c in Z_PASSES[q]:
+                    z_transpose(c)
+                for m in new:
+                    w_transpose(m)
+                for m in old:
+                    w_quantise(m)
             if q == 3:
                 times_x2(0)
             for c in Z_PASSES[q][::2]:

from contextlib import ExitStack

import concourse.mybir as mybir
from concourse.masks import make_identity

F32 = mybir.dt.float32
BF16 = mybir.dt.bfloat16
U32 = mybir.dt.uint32
U8 = mybir.dt.uint8
I32 = mybir.dt.int32
FP8X4 = mybir.dt.float8_e4m3fn_x4
ALU = mybir.AluOpType

P = 128
B, K, R, O = 256, 4096, 1024, 128
HALVES = B // P
PASS = 512
STACKS = 4
TILES = 8
TILE_K = 22 * 64
TILE_STEP = 6 * 64
ROWS = P // STACKS
PAIR_STEP = ROWS * K + TILE_STEP

FLOPS = 2 * B * K * R + 2 * B * R * O
BYTES = 2 * B * K + 2 * 2 * 856064 + 2 * 2 * B * R + 2 * O * R + 2 * O + 4 * B * O

Z_PASSES = ((0, 1, 2, 3), (4, 5), (), (6, 7), ())


def first_pass(m):
    return (TILE_STEP * m) // PASS


def n_passes(m):
    return (TILE_STEP * m + TILE_K - 1) // PASS - first_pass(m) + 1


def lead(m):
    return TILE_STEP * m - PASS * first_pass(m)


def tile_chebyshev_l3_sparsed32_stack_pb_kernel(tc, z, T3, mask, x1, x2, C_w, C_b, out):
    nc = tc.nc
    with ExitStack() as ctx:
        keep = ctx.enter_context(tc.tile_pool(name="keep", bufs=1))
        acc = ctx.enter_context(tc.psum_pool(name="acc", bufs=1))
        turn = ctx.enter_context(tc.psum_pool(name="turn", bufs=4))
        ctx.enter_context(tc.manual_schedule())

        ident_f = keep.tile([P, P], F32, name="ident_f")
        ident_b = keep.tile([P, P], BF16, name="ident_b")
        ones = keep.tile([P, P], BF16, name="ones")
        bias_row = keep.tile([P, O], BF16, name="bias_row")
        bias_all = keep.tile([P, O], F32, name="bias_all")

        z_in = [keep.tile([P, HALVES * 2 * PASS], BF16, name="z_in_%d" % j) for j in range(4)]
        z_grouped = keep.tile([P, 8 * B * 4], BF16, name="z_grouped", align_bytes=64)
        z_codes = keep.tile([P, 8 * B], U32, name="z_codes", align_bytes=64)
        z_scales = keep.tile([P, 8 * B], U8, name="z_scales", align_bytes=64)

        t3_in = [keep.tile([P, 2 * TILE_K], BF16, name="t3_in_%d" % q) for q in range(TILES // 2)]
        mask_in = [keep.tile([P, 2 * TILE_K], BF16, name="mask_in_%d" % q) for q in range(TILES // 2)]
        w_masked = [keep.tile([P, PASS * n_passes(m)], BF16, name="w_masked_%d" % m) for m in range(TILES)]
        w_grouped = [
            keep.tile([P, PASS * n_passes(m)], BF16, name="w_grouped_%d" % m, align_bytes=64) for m in range(TILES)
        ]
        w_codes = [keep.tile([P, P * n_passes(m)], U32, name="w_codes_%d" % m, align_bytes=64) for m in range(TILES)]
        w_scales = [keep.tile([P, P * n_passes(m)], U8, name="w_scales_%d" % m, align_bytes=64) for m in range(TILES)]

        x1_in = keep.tile([P, HALVES * R], BF16, name="x1_in")
        x2_in = keep.tile([P, HALVES * R], BF16, name="x2_in")
        doubled = [[keep.tile([P, 512], F32, name="doubled_%d_%d" % (h, g)) for g in range(2)] for h in range(HALVES)]
        x3 = [[keep.tile([P, 512], BF16, name="x3_%d_%d" % (h, g)) for g in range(2)] for h in range(HALVES)]
        x3_grouped = keep.tile([P, HALVES * 2 * PASS], BF16, name="x3_grouped", align_bytes=64)
        x3_codes = keep.tile([P, HALVES * 2 * P], U32, name="x3_codes", align_bytes=64)
        x3_scales = keep.tile([P, HALVES * 2 * P], U8, name="x3_scales", align_bytes=64)

        cw_in = keep.tile([P, R], BF16, name="cw_in")
        cw_grouped = keep.tile([P, 2 * PASS], BF16, name="cw_grouped", align_bytes=64)
        cw_codes = keep.tile([P, 2 * P], U32, name="cw_codes", align_bytes=64)
        cw_scales = keep.tile([P, 2 * P], U8, name="cw_scales", align_bytes=64)
        result = [keep.tile([P, O], F32, name="result_%d" % h) for h in range(HALVES)]

        p3 = [[acc.tile([P, 512], F32, name="p3_%d_%d" % (h, g)) for g in range(2)] for h in range(HALVES)]

        nc.vector.memset(bias_row[:], 0.0)
        nc.scalar.dma_start(out=bias_row[0:1, :], in_=C_b.unsqueeze(0))
        make_identity(nc, ident_f[:])
        make_identity(nc, ident_b[:])
        nc.vector.memset(ones[:], 1.0)
        for m in range(TILES):
            if lead(m) > 0:
                nc.vector.memset(w_masked[m][:, 0:lead(m)].bitcast(I32), 0)
            if lead(m) + TILE_K < PASS * n_passes(m):
                nc.vector.memset(w_masked[m][:, lead(m) + TILE_K:PASS * n_passes(m)].bitcast(I32), 0)

        def load_z(j):
            cols = slice(2 * PASS * j, 2 * PASS * (j + 1))
            nc.sync.dma_start(
                out=z_in[j][:].rearrange("p (h k) -> p h k", h=HALVES),
                in_=z.rearrange("(h p) k -> p h k", h=HALVES)[:, :, cols],
            )

        def load_one_tile(src, dst, m, s):
            rows = slice(256 * s + ROWS * m, 256 * s + ROWS * (m + 1))
            nc.sync.dma_start(
                out=dst[m // 2][s:P:STACKS, TILE_K * (m % 2):TILE_K * (m % 2 + 1)],
                in_=src[rows, TILE_STEP * m:TILE_STEP * m + TILE_K],
            )

        def load_two_tiles(q):
            m = 2 * q
            for src, dst in ((T3, t3_in), (mask, mask_in)):
                for s in range(STACKS):
                    start = (256 * s + ROWS * m) * K + TILE_STEP * m
                    if start + 2 * PAIR_STEP <= R * K:
                        both = src.rearrange("r k -> (r k)")[start:start + 2 * PAIR_STEP]
                        both = both.rearrange("(t x) -> t x", t=2)[:, 0:ROWS * K]
                        both = both.rearrange("t (c k) -> c t k", k=K)[:, :, 0:TILE_K]
                        nc.sync.dma_start(out=dst[q][s:P:STACKS, :].rearrange("c (t k) -> c t k", t=2), in_=both)
                    else:
                        load_one_tile(src, dst, m, s)
                        load_one_tile(src, dst, m + 1, s)

        def load_halves(dst, src):
            nc.sync.dma_start(
                out=dst[:].rearrange("p (h r) -> p h r", h=HALVES), in_=src.rearrange("(h p) r -> p h r", h=HALVES)
            )

        load_two_tiles(0)
        load_z(0)
        load_z(1)
        load_two_tiles(1)
        load_z(2)
        load_two_tiles(2)
        for m in (6, 7):
            for src, dst in ((T3, t3_in), (mask, mask_in)):
                for s in range(STACKS):
                    load_one_tile(src, dst, m, s)
        load_z(3)
        load_halves(x2_in, x2)
        nc.sync.dma_start(out=cw_in[:], in_=C_w)
        load_halves(x1_in, x1)

        def z_transpose(c):
            words = z_in[c // 2][:].bitcast(F32)
            bank = turn.tile([P, 512], F32, name="z_t", tag="turn")
            for u in range(2):
                for h in range(HALVES):
                    first = PASS * h + 256 * (c % 2) + P * u
                    nc.tensor.transpose(bank[:, B * u + P * h:B * u + P * (h + 1)], words[:, first:first + P], ident_f[:])
            nc.scalar.copy(
                out=z_grouped[:].bitcast(F32)[:, 2 * B * c:2 * B * (c + 1)].rearrange("p (b u) -> p b u", u=2),
                in_=bank[:].rearrange("p (u b) -> p b u", u=2),
            )

        def z_quantise(c):
            nc.vector.quantize_mx(
                out=z_codes[:, B * c:B * (c + 2)].bitcast(FP8X4),
                scales=z_scales[:, B * c:B * (c + 2)],
                in_=z_grouped[:, 4 * B * c:4 * B * (c + 2)],
            )

        def w_multiply(m):
            cols = slice(TILE_K * (m % 2), TILE_K * (m % 2 + 1))
            nc.vector.tensor_tensor(
                out=w_masked[m][:, lead(m):lead(m) + TILE_K],
                in0=t3_in[m // 2][:, cols],
                in1=mask_in[m // 2][:, cols],
                op=ALU.mult,
            )

        def w_transpose(m):
            words = w_masked[m][:].bitcast(F32)
            grouped = w_grouped[m][:].bitcast(F32)
            for a in range(0, n_passes(m), 2):
                n = min(2, n_passes(m) - a)
                bank = turn.tile([P, 512], F32, name="w_t", tag="turn")
                for i in range(2 * n):
                    nc.tensor.transpose(bank[:, P * i:P * (i + 1)], words[:, 256 * a + P * i:256 * a + P * (i + 1)], ident_f[:])
                nc.scalar.copy(
                    out=grouped[:, 256 * a:256 * (a + n)].rearrange("p (a r u) -> p a r u", a=n, u=2),
                    in_=bank[:, 0:256 * n].rearrange("p (a u r) -> p a r u", a=n, u=2),
                )

        def w_quantise(m):
            for a, n in ((0, 4),) if n_passes(m) == 4 else ((0, 2), (2, 1)):
                nc.vector.quantize_mx(
                    out=w_codes[m][:, P * a:P * (a + n)].bitcast(FP8X4),
                    scales=w_scales[m][:, P * a:P * (a + n)],
                    in_=w_grouped[m][:, PASS * a:PASS * (a + n)],
                )

        def first_product(m):
            for h in range(HALVES):
                for a in range(n_passes(m)):
                    zcols = slice(B * (first_pass(m) + a) + P * h, B * (first_pass(m) + a) + P * (h + 1))
                    nc.tensor.matmul_mx(
                        out=p3[h][m // 4][:, P * (m % 4):P * (m % 4 + 1)],
                        lhsT=z_codes[:, zcols].bitcast(FP8X4),
                        lhsT_scale=z_scales[:, zcols],
                        rhs=w_codes[m][:, P * a:P * (a + 1)].bitcast(FP8X4),
                        rhs_scale=w_scales[m][:, P * a:P * (a + 1)],
                        start=(a == 0),
                        stop=(a == n_passes(m) - 1),
                    )

        def as_p3(t, h, g):
            return t[:, R * h:R * (h + 1)].rearrange("p (s g y) -> p g y s", s=STACKS, g=2)[:, g]

        def times_x2(g):
            for h in range(HALVES):
                nc.vector.scalar_tensor_tensor(
                    out=doubled[h][g][:].rearrange("p (y s) -> p y s", s=STACKS),
                    in0=p3[h][g][:].rearrange("p (y s) -> p y s", s=STACKS),
                    scalar=2.0,
                    in1=as_p3(x2_in, h, g),
                    op0=ALU.mult,
                    op1=ALU.mult,
                )

        def minus_x1(g):
            for h in range(HALVES):
                nc.vector.tensor_tensor(
                    out=x3[h][g][:].rearrange("p (s y) -> p y s", s=STACKS),
                    in0=doubled[h][g][:].rearrange("p (y s) -> p y s", s=STACKS),
                    in1=as_p3(x1_in, h, g),
                    op=ALU.subtract,
                )

        def spread_bias():
            bank = turn.tile([P, O], F32, name="bias_t", tag="turn")
            nc.tensor.matmul(bank[:], lhsT=ones[:], rhs=bias_row[:], start=True, stop=True)
            nc.scalar.copy(out=bias_all[:], in_=bank[:])

        def cw_transpose():
            bank = turn.tile([P, R], BF16, name="cw_t", tag="turn")
            for a in range(R // P):
                nc.tensor.transpose(bank[:, P * a:P * (a + 1)], cw_in[:, P * a:P * (a + 1)], ident_b[:])
            nc.scalar.copy(
                out=cw_grouped[:].rearrange("p (g o t) -> p g o t", g=2, t=4),
                in_=bank[:].rearrange("p (g t o) -> p g o t", g=2, t=4),
            )

        def cw_quantise():
            nc.vector.quantize_mx(out=cw_codes[:].bitcast(FP8X4), scales=cw_scales[:], in_=cw_grouped[:])

        x3_t = {}

        def x3_transpose(g):
            for h in range(HALVES):
                for big in range(2):
                    if (big, h) not in x3_t:
                        if h == 0:
                            x3_t[(big, h)] = acc.tile([P, 512], BF16, name="x3_t_%d_0" % big, tag="p3_%d_0" % big)
                        else:
                            x3_t[(big, h)] = turn.tile([P, 512], BF16, name="x3_t_%d_1" % big, tag="turn")
                for s in range(STACKS):
                    a = 2 * s + g
                    nc.tensor.transpose(x3_t[(a // 4, h)][:, P * (a % 4):P * (a % 4 + 1)], x3[h][g][:, P * s:P * (s + 1)], ident_b[:])

        def x3_group(h):
            for big, copy in ((0, nc.scalar.copy), (1, nc.vector.tensor_copy)):
                first = 2 * PASS * h + PASS * big
                copy(
                    out=x3_grouped[:, first:first + PASS].rearrange("p (b t) -> p b t", t=4),
                    in_=x3_t[(big, h)][:].rearrange("p (t b) -> p b t", t=4),
                )

        def x3_quantise(h):
            nc.vector.quantize_mx(
                out=x3_codes[:, 2 * P * h:2 * P * (h + 1)].bitcast(FP8X4),
                scales=x3_scales[:, 2 * P * h:2 * P * (h + 1)],
                in_=x3_grouped[:, 2 * PASS * h:2 * PASS * (h + 1)],
            )

        def head(h):
            bank = turn.tile([P, O], F32, name="out_t", tag="turn")
            for big in range(2):
                cols = slice(2 * P * h + P * big, 2 * P * h + P * (big + 1))
                nc.tensor.matmul_mx(
                    out=bank[:],
                    lhsT=x3_codes[:, cols].bitcast(FP8X4),
                    lhsT_scale=x3_scales[:, cols],
                    rhs=cw_codes[:, P * big:P * (big + 1)].bitcast(FP8X4),
                    rhs_scale=cw_scales[:, P * big:P * (big + 1)],
                    start=(big == 0),
                    stop=(big == 1),
                )
            nc.vector.tensor_tensor(out=result[h][:], in0=bank[:], in1=bias_all[:], op=ALU.add)
            nc.sync.dma_start(out=out[P * h:P * (h + 1), :], in_=result[h][:])

        spread_bias()
        for q in range(TILES // 2 + 1):
            new = (2 * q, 2 * q + 1) if q < TILES // 2 else ()
            old = (2 * q - 2, 2 * q - 1) if q > 0 else ()
            if q == 3:
                w_multiply(6)
                w_transpose(6)
                for m in old:
                    w_quantise(m)
                w_multiply(7)
                for c in Z_PASSES[q]:
                    z_transpose(c)
                w_transpose(7)
            else:
                for m in new:
                    w_multiply(m)
                for c in Z_PASSES[q]:
                    z_transpose(c)
                for m in new:
                    w_transpose(m)
                for m in old:
                    w_quantise(m)
            if q == 3:
                times_x2(0)
            for c in Z_PASSES[q][::2]:
                z_quantise(c)
            for m in old:
                first_product(m)
        cw_transpose()
        minus_x1(0)
        x3_transpose(0)
        times_x2(1)
        minus_x1(1)
        cw_quantise()
        x3_transpose(1)
        for h in range(HALVES):
            x3_group(h)
        for h in range(HALVES):
            x3_quantise(h)
        for h in range(HALVES):
            head(h)
